import numpy as np
import ml_dtypes


def mxq(x, axis, fmt="e4m3"):
    dtype, down = {"e4m3": (ml_dtypes.float8_e4m3fn, 7), "e5m2": (ml_dtypes.float8_e5m2, 14)}[fmt]
    v = np.moveaxis(np.asarray(x, np.float32).astype(ml_dtypes.bfloat16).astype(np.float64), axis, -1)
    blocks = v.reshape(v.shape[:-1] + (-1, 32))
    amax = np.abs(blocks).max(-1, keepdims=True)
    byte = np.maximum(np.where(amax > 0, np.frexp(amax)[1] - 1 + 127, 0) - down, 1)
    scale = np.exp2(byte - 127.0)
    codes = (blocks / scale).astype(np.float32).astype(dtype).astype(np.float64)
    return np.moveaxis((codes * scale).reshape(v.shape), -1, axis)


WIDE = False


def mx_kscale(k):
    if not WIDE:
        return np.ones(k)
    levels = np.array([10, -10, 5, -5, 0])
    a = np.random.permutation(np.resize(levels, k // 512 * 4)).reshape(k // 512, 4)
    idx = np.arange(k)
    return np.exp2(a[idx // 512, idx % 128 // 32])


BF16 = ml_dtypes.bfloat16


def bf(x):
    return np.asarray(x, np.float32).astype(BF16)


def f64(x):
    return np.asarray(x).astype(np.float64)


B, C, D, H, W, W0, W1 = 2, 512, 128, 32, 32, 64, 256
N = H * W


def setup_inputs():
    s = mx_kscale(C)
    return {
        "x": bf(np.random.standard_normal((B, C, N))),
        "out1": bf(np.random.standard_normal((B, C, N)) * 0.6 * s[None, :, None]),
        "q": bf(np.random.standard_normal((B, N, D)) * 0.42),
        "k": bf(np.random.standard_normal((B, D, N)) * 0.42),
        "wv2": bf(np.random.standard_normal((C, C)) * 4.0 / np.sqrt(C) / s[None, :]),
        "bv2": bf(np.random.standard_normal(C) * 0.3),
        "gamma": bf(1.0 + 0.1 * np.random.standard_normal(1)),
    }


def reference(x, out1, q, k, wv2, bv2, gamma):
    val = (mxq(f64(wv2), 1, "e4m3") @ mxq(f64(out1), 1, "e4m3")) + f64(bv2)[None, :, None]
    s = f64(q) @ f64(k)
    e = np.exp(s - s.max(-1, keepdims=True))
    out = (mxq(val, 2, "e4m3") @ mxq(e, 2, "e4m3").transpose(0, 2, 1)) / e.sum(-1)[:, None, :]
    return f64(gamma)[0] * out + f64(x)

@@ -1,0 +1,275 @@
+from contextlib import ExitStack
+
+import concourse.mybir as mybir
+from concourse.masks import make_identity
+
+F32 = mybir.dt.float32
+BF16 = mybir.dt.bfloat16
+U32 = mybir.dt.uint32
+U8 = mybir.dt.uint8
+FP8X4 = mybir.dt.float8_e4m3fn_x4
+ALU = mybir.AluOpType
+ACT = mybir.ActivationFunctionType
+AXIS_X = mybir.AxisListType.X
+
+B, C, D, N = 2, 512, 128, 1024
+P = 128
+PACK = 4
+K_PASS = P * PACK
+BANK = 512
+C_TILES = C // P
+M_TILES = N // P
+KEY_PASSES = N // K_PASS
+KEY_BANKS = N // BANK
+STORE_TILES = 2
+
+FLOPS = 2 * B * (C * C * N + N * D * N + C * N * N)
+
+
+def tile_mvpam_module_mask_cascade_pb_kernel(tc, x, out1, q, k, wv2, bv2, gamma, out):
+    nc = tc.nc
+    with ExitStack() as ctx:
+        const = ctx.enter_context(tc.tile_pool(name="const", bufs=1))
+        per_batch = ctx.enter_context(tc.tile_pool(name="per_batch", bufs=B))
+        work = ctx.enter_context(tc.tile_pool(name="work", bufs=4))
+        ps_scores = ctx.enter_context(tc.psum_pool(name="ps_scores", bufs=2))
+        ps_turn = ctx.enter_context(tc.psum_pool(name="ps_turn", bufs=2))
+        ps_mx = ctx.enter_context(tc.psum_pool(name="ps_mx", bufs=2))
+
+        q_sb, k_sb, o1_sb, x_sb = [], [], [], []
+
+        def load_scores_inputs(b):
+            q_rows = per_batch.tile([P, M_TILES, D], BF16)
+            nc.sync.dma_start(out=q_rows[:], in_=q[b].rearrange("(i p) d -> p i d", p=P))
+            q_sb.append(q_rows)
+            k_rows = per_batch.tile([P, N], BF16)
+            nc.sync.dma_start(out=k_rows[:], in_=k[b])
+            k_sb.append(k_rows)
+
+        def load_out1(b):
+            o1_rows = per_batch.tile([P, PACK, N], BF16)
+            nc.sync.dma_start(out=o1_rows[:], in_=out1[b].rearrange("(t p) n -> p t n", p=P))
+            o1_sb.append(o1_rows)
+
+        def load_x(b):
+            x_rows = per_batch.tile([P, C_TILES, N], BF16)
+            nc.sync.dma_start(out=x_rows[:], in_=x[b].rearrange("(ct p) m -> p ct m", p=P))
+            x_sb.append(x_rows)
+
+        load_scores_inputs(0)
+        w_sb = const.tile([P, C_TILES, C], BF16)
+        nc.sync.dma_start(out=w_sb[:], in_=wv2.rearrange("(ct p) ci -> p ct ci", p=P))
+        load_out1(0)
+        bias_bc = const.tile([P, C], BF16)
+        nc.sync.dma_start(out=bias_bc[:], in_=bv2.partition_broadcast(P))
+        gamma_bf = const.tile([P, 1], BF16)
+        nc.sync.dma_start(out=gamma_bf[:], in_=gamma.partition_broadcast(P))
+        load_x(0)
+        load_scores_inputs(1)
+        load_out1(1)
+        load_x(1)
+
+        ident_bf = const.tile([P, P], BF16)
+        make_identity(nc, ident_bf[:])
+        ident_f32 = const.tile([P, P], F32)
+        make_identity(nc, ident_f32[:])
+        zero_col = const.tile([P, 1], F32)
+        nc.vector.memset(zero_col[:], 0.0)
+        one_col = const.tile([P, 1], F32)
+        nc.scalar.activation(out=one_col[:], in_=zero_col[:], func=ACT.Exp)
+        gamma_f32 = const.tile([P, 1], F32)
+        nc.vector.tensor_copy(out=gamma_f32[:], in_=gamma_bf[:])
+
+        qT_sb = []
+
+        def turn_queries(b):
+            qT_ps = ps_turn.tile([P, M_TILES, P], BF16, tag="turn")
+            for i in range(M_TILES):
+                nc.tensor.transpose(qT_ps[:, i, :], q_sb[b][:, i, :], ident_bf[:])
+            qT = per_batch.tile([P, N], BF16)
+            nc.scalar.copy(out=qT[:], in_=qT_ps[:].rearrange("d i m -> d (i m)"))
+            qT_sb.append(qT)
+
+        turn_queries(0)
+
+        w_grp = const.tile([P, C, PACK], BF16, align_bytes=64)
+        for ct in range(C_TILES):
+            wT_ps = ps_turn.tile([P, PACK, P], BF16, tag="turn")
+            for t in range(PACK):
+                nc.tensor.transpose(wT_ps[:, t, :], w_sb[:, ct, t * P : (t + 1) * P], ident_bf[:])
+            nc.scalar.copy(
+                out=w_grp[:, ct * P : (ct + 1) * P, :], in_=wT_ps[:].rearrange("p t c -> p c t")
+            )
+        w_codes = const.tile([P, C], U32, align_bytes=64)
+        w_scales = const.tile([P, C], U8, align_bytes=64)
+        nc.vector.quantize_mx(
+            out=w_codes[:].bitcast(FP8X4),
+            scales=w_scales[:],
+            in_=w_grp[:].rearrange("p c t -> p (c t)"),
+        )
+
+        values = []
+
+        def new_values(b):
+            o1_grp = per_batch.tile([P, N, PACK], BF16, align_bytes=64)
+            o1_codes = per_batch.tile([P, N], U32, align_bytes=64)
+            o1_scales = per_batch.tile([P, N], U8, align_bytes=64)
+            v_grp = per_batch.tile([P, KEY_PASSES, C, PACK], BF16, align_bytes=64)
+            v_codes = per_batch.tile([P, KEY_PASSES, C], U32, align_bytes=64)
+            v_scales = per_batch.tile([P, KEY_PASSES, C], U8, align_bytes=64)
+            values.append(
+                {
+                    "o1_grp": o1_grp,
+                    "o1_codes": o1_codes,
+                    "o1_scales": o1_scales,
+                    "v_grp": v_grp,
+                    "v_codes": v_codes,
+                    "v_scales": v_scales,
+                }
+            )
+
+        def values_piece(b, g, cb):
+            v = values[b]
+            keys = slice(g * K_PASS, (g + 1) * K_PASS)
+            if cb == 0:
+                nc.vector.tensor_copy(
+                    out=v["o1_grp"][:, keys, :].rearrange("p (c i) t -> p c t i", i=4),
+                    in_=o1_sb[b][:, :, keys].rearrange("p t (c i) -> p c t i", i=4),
+                )
+                nc.vector.quantize_mx(
+                    out=v["o1_codes"][:, keys].bitcast(FP8X4),
+                    scales=v["o1_scales"][:, keys],
+                    in_=v["o1_grp"][:, keys, :].rearrange("p n t -> p (n t)"),
+                )
+            chans = slice(cb * P, (cb + 1) * P)
+            vT_ps = ps_mx.tile([P, PACK, P], F32, tag="mx")
+            for t in range(PACK):
+                key_tile = slice(g * K_PASS + t * P, g * K_PASS + (t + 1) * P)
+                nc.tensor.matmul_mx(
+                    out=vT_ps[:, t, :],
+                    lhsT=v["o1_codes"][:, key_tile].bitcast(FP8X4),
+                    lhsT_scale=v["o1_scales"][:, key_tile],
+                    rhs=w_codes[:, chans].bitcast(FP8X4),
+                    rhs_scale=w_scales[:, chans],
+                    start=True,
+                    stop=True,
+                )
+            nc.vector.tensor_tensor(
+                out=v["v_grp"][:, g, chans, :],
+                in0=vT_ps[:].rearrange("p t c -> p c t"),
+                in1=bias_bc[:, chans].unsqueeze(2).to_broadcast([P, P, PACK]),
+                op=ALU.add,
+            )
+            if cb == C_TILES - 1:
+                nc.vector.quantize_mx(
+                    out=v["v_codes"][:, g, :].bitcast(FP8X4),
+                    scales=v["v_scales"][:, g, :],
+                    in_=v["v_grp"][:, g, :, :].rearrange("p c t -> p (c t)"),
+                )
+
+        new_values(0)
+        for g in range(KEY_PASSES):
+            for cb in range(C_TILES):
+                values_piece(0, g, cb)
+
+        for b in range(B):
+            if b + 1 < B:
+                turn_queries(b + 1)
+                new_values(b + 1)
+            out_view = out[b].rearrange("(ct p) m -> p ct m", p=P)
+            for i in range(M_TILES):
+                queries = slice(i * P, (i + 1) * P)
+
+                s_ps = ps_scores.tile([P, KEY_BANKS, BANK], F32)
+                for h in range(KEY_BANKS):
+                    nc.tensor.matmul(
+                        out=s_ps[:, h, :],
+                        lhsT=qT_sb[b][:, queries],
+                        rhs=k_sb[b][:, h * BANK : (h + 1) * BANK],
+                        start=True,
+                        stop=True,
+                    )
+                bank_max = work.tile([P, KEY_BANKS], F32)
+                for h in range(KEY_BANKS):
+                    nc.vector.tensor_reduce(
+                        out=bank_max[:, h : h + 1], in_=s_ps[:, h, :], axis=AXIS_X, op=ALU.max
+                    )
+                neg_max = work.tile([P, 1], F32)
+                nc.vector.tensor_scalar(
+                    out=neg_max[:],
+                    in0=bank_max[:, 0:1],
+                    scalar1=bank_max[:, 1:2],
+                    scalar2=-1.0,
+                    op0=ALU.max,
+                    op1=ALU.mult,
+                )
+                e_sb = work.tile([P, N], BF16)
+                bank_sum = work.tile([P, KEY_BANKS], F32)
+                for h in range(KEY_BANKS):
+                    nc.scalar.activation(
+                        out=e_sb[:, h * BANK : (h + 1) * BANK],
+                        in_=s_ps[:, h, :],
+                        func=ACT.Exp,
+                        bias=neg_max[:],
+                        scale=1.0,
+                        accum_out=bank_sum[:, h : h + 1],
+                    )
+                row_sum = work.tile([P, 1], F32)
+                nc.vector.tensor_tensor(
+                    out=row_sum[:], in0=bank_sum[:, 0:1], in1=bank_sum[:, 1:2], op=ALU.add
+                )
+                inv_sum = work.tile([P, 1], F32)
+                nc.vector.reciprocal(out=inv_sum[:], in_=row_sum[:])
+
+                eT_ps = ps_turn.tile([P, KEY_PASSES * PACK, P], BF16, tag="turn")
+                for j in range(KEY_PASSES * PACK):
+                    nc.tensor.transpose(eT_ps[:, j, :], e_sb[:, j * P : (j + 1) * P], ident_bf[:])
+                e_grp = work.tile([P, KEY_PASSES, P, PACK], BF16, align_bytes=64)
+                nc.scalar.copy(
+                    out=e_grp[:], in_=eT_ps[:].rearrange("p (g t) m -> p g m t", g=KEY_PASSES)
+                )
+                e_codes = work.tile([P, KEY_PASSES, P], U32, align_bytes=64)
+                e_scales = work.tile([P, KEY_PASSES, P], U8, align_bytes=64)
+                nc.vector.quantize_mx(
+                    out=e_codes[:].rearrange("p g m -> p (g m)").bitcast(FP8X4),
+                    scales=e_scales[:].rearrange("p g m -> p (g m)"),
+                    in_=e_grp[:].rearrange("p g m t -> p (g m t)"),
+                )
+
+                attT_ps = ps_mx.tile([P, C], F32, tag="mx")
+                for g in range(KEY_PASSES):
+                    nc.tensor.matmul_mx(
+                        out=attT_ps[:],
+                        lhsT=e_codes[:, g, :].bitcast(FP8X4),
+                        lhsT_scale=e_scales[:, g, :],
+                        rhs=values[b]["v_codes"][:, g, :].bitcast(FP8X4),
+                        rhs_scale=values[b]["v_scales"][:, g, :],
+                        start=(g == 0),
+                        stop=(g == KEY_PASSES - 1),
+                    )
+                attT_sb = work.tile([P, C], F32)
+                nc.scalar.activation(out=attT_sb[:], in_=attT_ps[:], func=ACT.Copy, scale=inv_sum[:])
+                att_ps = ps_turn.tile([P, C_TILES, P], F32, tag="turn")
+                for ct in range(C_TILES):
+                    nc.tensor.transpose(
+                        att_ps[:, ct, :], attT_sb[:, ct * P : (ct + 1) * P], ident_f32[:]
+                    )
+                part = i % STORE_TILES
+                if part == 0:
+                    out_sb = work.tile([P, C_TILES, STORE_TILES * P], F32)
+                nc.vector.scalar_tensor_tensor(
+                    out=out_sb[:, :, part * P : (part + 1) * P],
+                    in0=att_ps[:],
+                    scalar=gamma_f32[:],
+                    in1=x_sb[b][:, :, queries],
+                    op0=ALU.mult,
+                    op1=ALU.add,
+                )
+                if part == STORE_TILES - 1:
+                    first = (i - part) * P
+                    nc.sync.dma_start(
+                        out=out_view[:, :, first : first + STORE_TILES * P], in_=out_sb[:]
+                    )
+
+                if b + 1 < B:
+                    values_piece(b + 1, i // C_TILES, i % C_TILES)

@@ -19,9 +19,13 @@ K_PASS = P * PACK
 BANK = 512
 C_TILES = C // P
 M_TILES = N // P
+TILES = B * M_TILES
 KEY_PASSES = N // K_PASS
 KEY_BANKS = N // BANK
+PIECES = KEY_PASSES * C_TILES
 STORE_TILES = 2
+LAG = 3
+PIECE_LEAD = 2
 
 FLOPS = 2 * B * (C * C * N + N * D * N + C * N * N)
 
@@ -29,6 +33,7 @@ FLOPS = 2 * B * (C * C * N + N * D * N + C * N * N)
 def tile_mvpam_module_mask_cascade_pb_kernel(tc, x, out1, q, k, wv2, bv2, gamma, out):
     nc = tc.nc
     with ExitStack() as ctx:
+        ctx.enter_context(tc.manual_schedule())
         const = ctx.enter_context(tc.tile_pool(name="const", bufs=1))
         per_batch = ctx.enter_context(tc.tile_pool(name="per_batch", bufs=B))
         work = ctx.enter_context(tc.tile_pool(name="work", bufs=4))
@@ -64,9 +69,9 @@ def tile_mvpam_module_mask_cascade_pb_kernel(tc, x, out1, q, k, wv2, bv2, gamma,
         nc.sync.dma_start(out=bias_bc[:], in_=bv2.partition_broadcast(P))
         gamma_bf = const.tile([P, 1], BF16)
         nc.sync.dma_start(out=gamma_bf[:], in_=gamma.partition_broadcast(P))
-        load_x(0)
         load_scores_inputs(1)
         load_out1(1)
+        load_x(0)
         load_x(1)
 
         ident_bf = const.tile([P, P], BF16)
@@ -77,8 +82,6 @@ def tile_mvpam_module_mask_cascade_pb_kernel(tc, x, out1, q, k, wv2, bv2, gamma,
         nc.vector.memset(zero_col[:], 0.0)
         one_col = const.tile([P, 1], F32)
         nc.scalar.activation(out=one_col[:], in_=zero_col[:], func=ACT.Exp)
-        gamma_f32 = const.tile([P, 1], F32)
-        nc.vector.tensor_copy(out=gamma_f32[:], in_=gamma_bf[:])
 
         qT_sb = []
 
@@ -90,27 +93,31 @@ def tile_mvpam_module_mask_cascade_pb_kernel(tc, x, out1, q, k, wv2, bv2, gamma,
             nc.scalar.copy(out=qT[:], in_=qT_ps[:].rearrange("d i m -> d (i m)"))
             qT_sb.append(qT)
 
-        turn_queries(0)
-
         w_grp = const.tile([P, C, PACK], BF16, align_bytes=64)
-        for ct in range(C_TILES):
-            wT_ps = ps_turn.tile([P, PACK, P], BF16, tag="turn")
-            for t in range(PACK):
-                nc.tensor.transpose(wT_ps[:, t, :], w_sb[:, ct, t * P : (t + 1) * P], ident_bf[:])
-            nc.scalar.copy(
-                out=w_grp[:, ct * P : (ct + 1) * P, :], in_=wT_ps[:].rearrange("p t c -> p c t")
-            )
         w_codes = const.tile([P, C], U32, align_bytes=64)
         w_scales = const.tile([P, C], U8, align_bytes=64)
-        nc.vector.quantize_mx(
-            out=w_codes[:].bitcast(FP8X4),
-            scales=w_scales[:],
-            in_=w_grp[:].rearrange("p c t -> p (c t)"),
-        )
+
+        def turn_weights():
+            for ct in range(C_TILES):
+                wT_ps = ps_turn.tile([P, PACK, P], BF16, tag="turn")
+                for t in range(PACK):
+                    nc.tensor.transpose(
+                        wT_ps[:, t, :], w_sb[:, ct, t * P : (t + 1) * P], ident_bf[:]
+                    )
+                nc.scalar.copy(
+                    out=w_grp[:, ct * P : (ct + 1) * P, :],
+                    in_=wT_ps[:].rearrange("p t c -> p c t"),
+                )
+
+        def quantise_weights():
+            nc.vector.quantize_mx(
+                out=w_codes[:].bitcast(FP8X4),
+                scales=w_scales[:],
+                in_=w_grp[:].rearrange("p c t -> p (c t)"),
+            )
 
         values = []
-
-        def new_values(b):
+        for b in range(B):
             o1_grp = per_batch.tile([P, N, PACK], BF16, align_bytes=64)
             o1_codes = per_batch.tile([P, N], U32, align_bytes=64)
             o1_scales = per_batch.tile([P, N], U8, align_bytes=64)
@@ -127,149 +134,268 @@ def tile_mvpam_module_mask_cascade_pb_kernel(tc, x, out1, q, k, wv2, bv2, gamma,
                     "v_scales": v_scales,
                 }
             )
+        vT_banks = {}
 
-        def values_piece(b, g, cb):
-            v = values[b]
+        def regroup_out1(b, g, copy):
             keys = slice(g * K_PASS, (g + 1) * K_PASS)
-            if cb == 0:
-                nc.vector.tensor_copy(
-                    out=v["o1_grp"][:, keys, :].rearrange("p (c i) t -> p c t i", i=4),
-                    in_=o1_sb[b][:, :, keys].rearrange("p t (c i) -> p c t i", i=4),
-                )
-                nc.vector.quantize_mx(
-                    out=v["o1_codes"][:, keys].bitcast(FP8X4),
-                    scales=v["o1_scales"][:, keys],
-                    in_=v["o1_grp"][:, keys, :].rearrange("p n t -> p (n t)"),
-                )
+            copy(
+                out=values[b]["o1_grp"][:, keys, :].rearrange("p (c i) t -> p c t i", i=4),
+                in_=o1_sb[b][:, :, keys].rearrange("p t (c i) -> p c t i", i=4),
+            )
+
+        def quantise_out1(b, g):
+            keys = slice(g * K_PASS, (g + 1) * K_PASS)
+            nc.vector.quantize_mx(
+                out=values[b]["o1_codes"][:, keys].bitcast(FP8X4),
+                scales=values[b]["o1_scales"][:, keys],
+                in_=values[b]["o1_grp"][:, keys, :].rearrange("p n t -> p (n t)"),
+            )
+
+        def values_matmul(b, piece):
+            if not 0 <= piece < PIECES:
+                return
+            g, cb = divmod(piece, C_TILES)
             chans = slice(cb * P, (cb + 1) * P)
             vT_ps = ps_mx.tile([P, PACK, P], F32, tag="mx")
             for t in range(PACK):
                 key_tile = slice(g * K_PASS + t * P, g * K_PASS + (t + 1) * P)
                 nc.tensor.matmul_mx(
                     out=vT_ps[:, t, :],
-                    lhsT=v["o1_codes"][:, key_tile].bitcast(FP8X4),
-                    lhsT_scale=v["o1_scales"][:, key_tile],
+                    lhsT=values[b]["o1_codes"][:, key_tile].bitcast(FP8X4),
+                    lhsT_scale=values[b]["o1_scales"][:, key_tile],
                     rhs=w_codes[:, chans].bitcast(FP8X4),
                     rhs_scale=w_scales[:, chans],
                     start=True,
                     stop=True,
                 )
+            vT_banks[b, piece] = vT_ps
+
+        def values_add_bias(b, piece):
+            if not 0 <= piece < PIECES:
+                return
+            g, cb = divmod(piece, C_TILES)
+            chans = slice(cb * P, (cb + 1) * P)
             nc.vector.tensor_tensor(
-                out=v["v_grp"][:, g, chans, :],
-                in0=vT_ps[:].rearrange("p t c -> p c t"),
+                out=values[b]["v_grp"][:, g, chans, :],
+                in0=vT_banks[b, piece][:].rearrange("p t c -> p c t"),
                 in1=bias_bc[:, chans].unsqueeze(2).to_broadcast([P, P, PACK]),
                 op=ALU.add,
             )
-            if cb == C_TILES - 1:
-                nc.vector.quantize_mx(
-                    out=v["v_codes"][:, g, :].bitcast(FP8X4),
-                    scales=v["v_scales"][:, g, :],
-                    in_=v["v_grp"][:, g, :, :].rearrange("p c t -> p (c t)"),
+
+        def values_quantise(b, piece):
+            if not 0 <= piece < PIECES:
+                return
+            g, cb = divmod(piece, C_TILES)
+            chans = slice(cb * P, (cb + 1) * P)
+            nc.vector.quantize_mx(
+                out=values[b]["v_codes"][:, g, chans].bitcast(FP8X4),
+                scales=values[b]["v_scales"][:, g, chans],
+                in_=values[b]["v_grp"][:, g, chans, :].rearrange("p c t -> p (c t)"),
+            )
+
+        live = {}
+
+        def scores(t):
+            if not 0 <= t < TILES:
+                return
+            b, i = divmod(t, M_TILES)
+            s_ps = ps_scores.tile([P, KEY_BANKS, BANK], F32)
+            for h in range(KEY_BANKS):
+                nc.tensor.matmul(
+                    out=s_ps[:, h, :],
+                    lhsT=qT_sb[b][:, i * P : (i + 1) * P],
+                    rhs=k_sb[b][:, h * BANK : (h + 1) * BANK],
+                    start=True,
+                    stop=True,
+                )
+            live["s", t] = s_ps
+
+        def row_max(t):
+            if not 0 <= t < TILES:
+                return
+            bank_max = work.tile([P, KEY_BANKS], F32)
+            for h in range(KEY_BANKS):
+                nc.vector.tensor_reduce(
+                    out=bank_max[:, h : h + 1], in_=live["s", t][:, h, :], axis=AXIS_X, op=ALU.max
+                )
+            neg_max = work.tile([P, 1], F32)
+            nc.vector.tensor_scalar(
+                out=neg_max[:],
+                in0=bank_max[:, 0:1],
+                scalar1=bank_max[:, 1:2],
+                scalar2=-1.0,
+                op0=ALU.max,
+                op1=ALU.mult,
+            )
+            live["neg_max", t] = neg_max
+
+        def exponentials(t):
+            if not 0 <= t < TILES:
+                return
+            e_sb = work.tile([P, N], BF16)
+            bank_sum = work.tile([P, KEY_BANKS], F32)
+            for h in range(KEY_BANKS):
+                nc.scalar.activation(
+                    out=e_sb[:, h * BANK : (h + 1) * BANK],
+                    in_=live["s", t][:, h, :],
+                    func=ACT.Exp,
+                    bias=live["neg_max", t][:],
+                    scale=1.0,
+                    accum_out=bank_sum[:, h : h + 1],
+                )
+            live["e", t] = e_sb
+            live["bank_sum", t] = bank_sum
+
+        def turn_e(t):
+            if not 0 <= t < TILES:
+                return
+            eT_ps = ps_turn.tile([P, KEY_PASSES * PACK, P], BF16, tag="turn")
+            for j in range(KEY_PASSES * PACK):
+                nc.tensor.transpose(eT_ps[:, j, :], live["e", t][:, j * P : (j + 1) * P], ident_bf[:])
+            live["eT", t] = eT_ps
+
+        def group_e(t):
+            if not 0 <= t < TILES:
+                return
+            e_grp = work.tile([P, KEY_PASSES, P, PACK], BF16, align_bytes=64)
+            nc.scalar.copy(
+                out=e_grp[:], in_=live["eT", t][:].rearrange("p (g u) m -> p g m u", g=KEY_PASSES)
+            )
+            live["e_grp", t] = e_grp
+
+        def quantise_e(t):
+            if not 0 <= t < TILES:
+                return
+            row_sum = work.tile([P, 1], F32)
+            nc.vector.tensor_tensor(
+                out=row_sum[:],
+                in0=live["bank_sum", t][:, 0:1],
+                in1=live["bank_sum", t][:, 1:2],
+                op=ALU.add,
+            )
+            inv_sum = work.tile([P, 1], F32)
+            nc.vector.reciprocal(out=inv_sum[:], in_=row_sum[:])
+            live["inv_sum", t] = inv_sum
+            e_codes = work.tile([P, KEY_PASSES, P], U32, align_bytes=64)
+            e_scales = work.tile([P, KEY_PASSES, P], U8, align_bytes=64)
+            nc.vector.quantize_mx(
+                out=e_codes[:].rearrange("p g m -> p (g m)").bitcast(FP8X4),
+                scales=e_scales[:].rearrange("p g m -> p (g m)"),
+                in_=live["e_grp", t][:].rearrange("p g m u -> p (g m u)"),
+            )
+            live["e_codes", t] = e_codes
+            live["e_scales", t] = e_scales
+
+        def attend(t):
+            if not 0 <= t < TILES:
+                return
+            b = t // M_TILES
+            attT_ps = ps_mx.tile([P, C], F32, tag="mx")
+            for g in range(KEY_PASSES):
+                nc.tensor.matmul_mx(
+                    out=attT_ps[:],
+                    lhsT=live["e_codes", t][:, g, :].bitcast(FP8X4),
+                    lhsT_scale=live["e_scales", t][:, g, :],
+                    rhs=values[b]["v_codes"][:, g, :].bitcast(FP8X4),
+                    rhs_scale=values[b]["v_scales"][:, g, :],
+                    start=(g == 0),
+                    stop=(g == KEY_PASSES - 1),
+                )
+            live["attT_ps", t] = attT_ps
+
+        def normalise(t):
+            if not 0 <= t < TILES:
+                return
+            attT_sb = work.tile([P, C], F32)
+            nc.scalar.activation(
+                out=attT_sb[:], in_=live["attT_ps", t][:], func=ACT.Copy, scale=live["inv_sum", t][:]
+            )
+            live["attT_sb", t] = attT_sb
+
+        def turn_att(t):
+            if not 0 <= t < TILES:
+                return
+            att_ps = ps_turn.tile([P, C_TILES, P], F32, tag="turn")
+            for ct in range(C_TILES):
+                nc.tensor.transpose(
+                    att_ps[:, ct, :], live["attT_sb", t][:, ct * P : (ct + 1) * P], ident_f32[:]
+                )
+            live["att", t] = att_ps
+
+        def finish(t):
+            if not 0 <= t < TILES:
+                return
+            b, i = divmod(t, M_TILES)
+            part = i % STORE_TILES
+            if part == 0:
+                out_sb = work.tile([P, C_TILES, STORE_TILES * P], F32)
+                live["out", t // STORE_TILES] = out_sb
+            out_sb = live["out", t // STORE_TILES]
+            nc.vector.scalar_tensor_tensor(
+                out=out_sb[:, :, part * P : (part + 1) * P],
+                in0=live["att", t][:],
+                scalar=gamma_f32[:],
+                in1=x_sb[b][:, :, i * P : (i + 1) * P],
+                op0=ALU.mult,
+                op1=ALU.add,
+            )
+            if part == STORE_TILES - 1:
+                first = (i - part) * P
+                nc.sync.dma_start(
+                    out=out[b].rearrange("(ct p) m -> p ct m", p=P)[:, :, first : first + STORE_TILES * P],
+                    in_=out_sb[:],
                 )
 
-        new_values(0)
-        for g in range(KEY_PASSES):
-            for cb in range(C_TILES):
-                values_piece(0, g, cb)
+        turn_queries(0)
+        scores(0)
+        row_max(0)
+        scores(1)
+        row_max(1)
+        turn_weights()
+        regroup_out1(0, 0, nc.vector.tensor_copy)
+        regroup_out1(0, 1, nc.scalar.copy)
+        quantise_weights()
+        gamma_f32 = const.tile([P, 1], F32)
+        nc.vector.tensor_copy(out=gamma_f32[:], in_=gamma_bf[:])
+        exponentials(0)
+        exponentials(1)
+        regroup_out1(1, 0, nc.scalar.copy)
+        regroup_out1(1, 1, nc.scalar.copy)
 
-        for b in range(B):
-            if b + 1 < B:
-                turn_queries(b + 1)
-                new_values(b + 1)
-            out_view = out[b].rearrange("(ct p) m -> p ct m", p=P)
-            for i in range(M_TILES):
-                queries = slice(i * P, (i + 1) * P)
+        def values_half(b, g):
+            quantise_out1(b, g)
+            for piece in range(g * C_TILES, (g + 1) * C_TILES):
+                values_matmul(b, piece)
+                values_add_bias(b, piece)
+                if piece > g * C_TILES:
+                    values_quantise(b, piece - 1)
+            values_quantise(b, (g + 1) * C_TILES - 1)
 
-                s_ps = ps_scores.tile([P, KEY_BANKS, BANK], F32)
-                for h in range(KEY_BANKS):
-                    nc.tensor.matmul(
-                        out=s_ps[:, h, :],
-                        lhsT=qT_sb[b][:, queries],
-                        rhs=k_sb[b][:, h * BANK : (h + 1) * BANK],
-                        start=True,
-                        stop=True,
-                    )
-                bank_max = work.tile([P, KEY_BANKS], F32)
-                for h in range(KEY_BANKS):
-                    nc.vector.tensor_reduce(
-                        out=bank_max[:, h : h + 1], in_=s_ps[:, h, :], axis=AXIS_X, op=ALU.max
-                    )
-                neg_max = work.tile([P, 1], F32)
-                nc.vector.tensor_scalar(
-                    out=neg_max[:],
-                    in0=bank_max[:, 0:1],
-                    scalar1=bank_max[:, 1:2],
-                    scalar2=-1.0,
-                    op0=ALU.max,
-                    op1=ALU.mult,
-                )
-                e_sb = work.tile([P, N], BF16)
-                bank_sum = work.tile([P, KEY_BANKS], F32)
-                for h in range(KEY_BANKS):
-                    nc.scalar.activation(
-                        out=e_sb[:, h * BANK : (h + 1) * BANK],
-                        in_=s_ps[:, h, :],
-                        func=ACT.Exp,
-                        bias=neg_max[:],
-                        scale=1.0,
-                        accum_out=bank_sum[:, h : h + 1],
-                    )
-                row_sum = work.tile([P, 1], F32)
-                nc.vector.tensor_tensor(
-                    out=row_sum[:], in0=bank_sum[:, 0:1], in1=bank_sum[:, 1:2], op=ALU.add
-                )
-                inv_sum = work.tile([P, 1], F32)
-                nc.vector.reciprocal(out=inv_sum[:], in_=row_sum[:])
+        values_half(0, 0)
+        turn_e(0)
+        values_half(0, 1)
+        turn_queries(1)
+        scores(2)
+        group_e(0)
+        turn_e(1)
+        quantise_out1(1, 0)
+        row_max(2)
 
-                eT_ps = ps_turn.tile([P, KEY_PASSES * PACK, P], BF16, tag="turn")
-                for j in range(KEY_PASSES * PACK):
-                    nc.tensor.transpose(eT_ps[:, j, :], e_sb[:, j * P : (j + 1) * P], ident_bf[:])
-                e_grp = work.tile([P, KEY_PASSES, P, PACK], BF16, align_bytes=64)
-                nc.scalar.copy(
-                    out=e_grp[:], in_=eT_ps[:].rearrange("p (g t) m -> p g m t", g=KEY_PASSES)
-                )
-                e_codes = work.tile([P, KEY_PASSES, P], U32, align_bytes=64)
-                e_scales = work.tile([P, KEY_PASSES, P], U8, align_bytes=64)
-                nc.vector.quantize_mx(
-                    out=e_codes[:].rearrange("p g m -> p (g m)").bitcast(FP8X4),
-                    scales=e_scales[:].rearrange("p g m -> p (g m)"),
-                    in_=e_grp[:].rearrange("p g m t -> p (g m t)"),
-                )
-
-                attT_ps = ps_mx.tile([P, C], F32, tag="mx")
-                for g in range(KEY_PASSES):
-                    nc.tensor.matmul_mx(
-                        out=attT_ps[:],
-                        lhsT=e_codes[:, g, :].bitcast(FP8X4),
-                        lhsT_scale=e_scales[:, g, :],
-                        rhs=values[b]["v_codes"][:, g, :].bitcast(FP8X4),
-                        rhs_scale=values[b]["v_scales"][:, g, :],
-                        start=(g == 0),
-                        stop=(g == KEY_PASSES - 1),
-                    )
-                attT_sb = work.tile([P, C], F32)
-                nc.scalar.activation(out=attT_sb[:], in_=attT_ps[:], func=ACT.Copy, scale=inv_sum[:])
-                att_ps = ps_turn.tile([P, C_TILES, P], F32, tag="turn")
-                for ct in range(C_TILES):
-                    nc.tensor.transpose(
-                        att_ps[:, ct, :], attT_sb[:, ct * P : (ct + 1) * P], ident_f32[:]
-                    )
-                part = i % STORE_TILES
-                if part == 0:
-                    out_sb = work.tile([P, C_TILES, STORE_TILES * P], F32)
-                nc.vector.scalar_tensor_tensor(
-                    out=out_sb[:, :, part * P : (part + 1) * P],
-                    in0=att_ps[:],
-                    scalar=gamma_f32[:],
-                    in1=x_sb[b][:, :, queries],
-                    op0=ALU.mult,
-                    op1=ALU.add,
-                )
-                if part == STORE_TILES - 1:
-                    first = (i - part) * P
-                    nc.sync.dma_start(
-                        out=out_view[:, :, first : first + STORE_TILES * P], in_=out_sb[:]
-                    )
-
-                if b + 1 < B:
-                    values_piece(b + 1, i // C_TILES, i % C_TILES)
+        for r in range(2, TILES + LAG + 2):
+            back = r - LAG
+            piece = r - PIECE_LEAD
+            scores(r + 1)
+            exponentials(r)
+            finish(back - 2)
+            values_add_bias(1, piece - 1)
+            attend(back)
+            values_matmul(1, piece)
+            turn_att(back - 1)
+            group_e(r - 1)
+            turn_e(r)
+            normalise(back)
+            quantise_e(r - 2)
+            values_quantise(1, piece - 1)
+            if piece + 1 == C_TILES:
+                quantise_out1(1, 1)
+            row_max(r + 1)

@@ -15,6 +15,8 @@ AXIS_X = mybir.AxisListType.X
 B, C, D, N = 2, 512, 128, 1024
 P = 128
 PACK = 4
+PAIR = 2
+HALVES = PACK // PAIR
 K_PASS = P * PACK
 BANK = 512
 C_TILES = C // P
@@ -24,8 +26,9 @@ KEY_PASSES = N // K_PASS
 KEY_BANKS = N // BANK
 PIECES = KEY_PASSES * C_TILES
 STORE_TILES = 2
+FIRST_ROUND = 2
 LAG = 3
-PIECE_LEAD = 2
+PIECE_LEAD = FIRST_ROUND
 
 FLOPS = 2 * B * (C * C * N + N * D * N + C * N * N)
 
@@ -53,7 +56,10 @@ def tile_mvpam_module_mask_cascade_pb_kernel(tc, x, out1, q, k, wv2, bv2, gamma,
 
         def load_out1(b):
             o1_rows = per_batch.tile([P, PACK, N], BF16)
-            nc.sync.dma_start(out=o1_rows[:], in_=out1[b].rearrange("(t p) n -> p t n", p=P))
+            nc.sync.dma_start(
+                out=o1_rows[:].rearrange("p (j e) n -> p j e n", e=PAIR),
+                in_=out1[b].rearrange("(j p e) n -> p j e n", p=P, e=PAIR),
+            )
             o1_sb.append(o1_rows)
 
         def load_x(b):
@@ -93,27 +99,32 @@ def tile_mvpam_module_mask_cascade_pb_kernel(tc, x, out1, q, k, wv2, bv2, gamma,
             nc.scalar.copy(out=qT[:], in_=qT_ps[:].rearrange("d i m -> d (i m)"))
             qT_sb.append(qT)
 
-        w_grp = const.tile([P, C, PACK], BF16, align_bytes=64)
+        w_grp = const.tile([P, C, HALVES], F32, align_bytes=64)
         w_codes = const.tile([P, C], U32, align_bytes=64)
         w_scales = const.tile([P, C], U8, align_bytes=64)
 
         def turn_weights():
-            for ct in range(C_TILES):
-                wT_ps = ps_turn.tile([P, PACK, P], BF16, tag="turn")
-                for t in range(PACK):
-                    nc.tensor.transpose(
-                        wT_ps[:, t, :], w_sb[:, ct, t * P : (t + 1) * P], ident_bf[:]
-                    )
+            per_bank = BANK // (HALVES * P)
+            for first in range(0, C_TILES, per_bank):
+                wT_ps = ps_turn.tile([P, per_bank, HALVES, P], F32, tag="turn")
+                for a in range(per_bank):
+                    w_words = w_sb[:, first + a, :].bitcast(F32)
+                    for j in range(HALVES):
+                        nc.tensor.transpose(
+                            wT_ps[:, a, j, :], w_words[:, j * P : (j + 1) * P], ident_f32[:]
+                        )
                 nc.scalar.copy(
-                    out=w_grp[:, ct * P : (ct + 1) * P, :],
-                    in_=wT_ps[:].rearrange("p t c -> p c t"),
+                    out=w_grp[:, first * P : (first + per_bank) * P, :].rearrange(
+                        "p (a c) j -> p a c j", a=per_bank
+                    ),
+                    in_=wT_ps[:].rearrange("p a j c -> p a c j"),
                 )
 
         def quantise_weights():
             nc.vector.quantize_mx(
                 out=w_codes[:].bitcast(FP8X4),
                 scales=w_scales[:],
-                in_=w_grp[:].rearrange("p c t -> p (c t)"),
+                in_=w_grp[:].rearrange("p c j -> p (c j)").bitcast(BF16),
             )
 
         values = []
@@ -137,18 +148,19 @@ def tile_mvpam_module_mask_cascade_pb_kernel(tc, x, out1, q, k, wv2, bv2, gamma,
         vT_banks = {}
 
         def regroup_out1(b, g, copy):
-            keys = slice(g * K_PASS, (g + 1) * K_PASS)
-            copy(
-                out=values[b]["o1_grp"][:, keys, :].rearrange("p (c i) t -> p c t i", i=4),
-                in_=o1_sb[b][:, :, keys].rearrange("p t (c i) -> p c t i", i=4),
-            )
+            for j in range(HALVES):
+                keys = slice(g * K_PASS + j * PAIR * P, g * K_PASS + (j + 1) * PAIR * P)
+                copy(
+                    out=values[b]["o1_grp"][:, keys, :].rearrange("p (e q) u -> p e q u", e=PAIR),
+                    in_=o1_sb[b][:, :, keys].rearrange("p u (q e) -> p e q u", e=PAIR),
+                )
 
         def quantise_out1(b, g):
             keys = slice(g * K_PASS, (g + 1) * K_PASS)
             nc.vector.quantize_mx(
                 out=values[b]["o1_codes"][:, keys].bitcast(FP8X4),
                 scales=values[b]["o1_scales"][:, keys],
-                in_=values[b]["o1_grp"][:, keys, :].rearrange("p n t -> p (n t)"),
+                in_=values[b]["o1_grp"][:, keys, :].rearrange("p n u -> p (n u)"),
             )
 
         def values_matmul(b, piece):
@@ -157,10 +169,10 @@ def tile_mvpam_module_mask_cascade_pb_kernel(tc, x, out1, q, k, wv2, bv2, gamma,
             g, cb = divmod(piece, C_TILES)
             chans = slice(cb * P, (cb + 1) * P)
             vT_ps = ps_mx.tile([P, PACK, P], F32, tag="mx")
-            for t in range(PACK):
-                key_tile = slice(g * K_PASS + t * P, g * K_PASS + (t + 1) * P)
+            for u in range(PACK):
+                key_tile = slice(g * K_PASS + u * P, g * K_PASS + (u + 1) * P)
                 nc.tensor.matmul_mx(
-                    out=vT_ps[:, t, :],
+                    out=vT_ps[:, u, :],
                     lhsT=values[b]["o1_codes"][:, key_tile].bitcast(FP8X4),
                     lhsT_scale=values[b]["o1_scales"][:, key_tile],
                     rhs=w_codes[:, chans].bitcast(FP8X4),
@@ -177,7 +189,7 @@ def tile_mvpam_module_mask_cascade_pb_kernel(tc, x, out1, q, k, wv2, bv2, gamma,
             chans = slice(cb * P, (cb + 1) * P)
             nc.vector.tensor_tensor(
                 out=values[b]["v_grp"][:, g, chans, :],
-                in0=vT_banks[b, piece][:].rearrange("p t c -> p c t"),
+                in0=vT_banks[b, piece][:].rearrange("p u c -> p c u"),
                 in1=bias_bc[:, chans].unsqueeze(2).to_broadcast([P, P, PACK]),
                 op=ALU.add,
             )
@@ -186,12 +198,20 @@ def tile_mvpam_module_mask_cascade_pb_kernel(tc, x, out1, q, k, wv2, bv2, gamma,
             if not 0 <= piece < PIECES:
                 return
             g, cb = divmod(piece, C_TILES)
-            chans = slice(cb * P, (cb + 1) * P)
+            if cb < C_TILES - 1:
+                return
             nc.vector.quantize_mx(
-                out=values[b]["v_codes"][:, g, chans].bitcast(FP8X4),
-                scales=values[b]["v_scales"][:, g, chans],
-                in_=values[b]["v_grp"][:, g, chans, :].rearrange("p c t -> p (c t)"),
+                out=values[b]["v_codes"][:, g, :].bitcast(FP8X4),
+                scales=values[b]["v_scales"][:, g, :],
+                in_=values[b]["v_grp"][:, g, :, :].rearrange("p c u -> p (c u)"),
             )
+
+        def values_half(b, g):
+            quantise_out1(b, g)
+            for piece in range(g * C_TILES, (g + 1) * C_TILES):
+                values_matmul(b, piece)
+                values_add_bias(b, piece)
+                values_quantise(b, piece)
 
         live = {}
 
@@ -249,17 +269,18 @@ def tile_mvpam_module_mask_cascade_pb_kernel(tc, x, out1, q, k, wv2, bv2, gamma,
         def turn_e(t):
             if not 0 <= t < TILES:
                 return
-            eT_ps = ps_turn.tile([P, KEY_PASSES * PACK, P], BF16, tag="turn")
-            for j in range(KEY_PASSES * PACK):
-                nc.tensor.transpose(eT_ps[:, j, :], live["e", t][:, j * P : (j + 1) * P], ident_bf[:])
+            e_words = live["e", t][:].bitcast(F32)
+            eT_ps = ps_turn.tile([P, KEY_PASSES * HALVES, P], F32, tag="turn")
+            for gj in range(KEY_PASSES * HALVES):
+                nc.tensor.transpose(eT_ps[:, gj, :], e_words[:, gj * P : (gj + 1) * P], ident_f32[:])
             live["eT", t] = eT_ps
 
         def group_e(t):
             if not 0 <= t < TILES:
                 return
-            e_grp = work.tile([P, KEY_PASSES, P, PACK], BF16, align_bytes=64)
+            e_grp = work.tile([P, KEY_PASSES, P, HALVES], F32, align_bytes=64)
             nc.scalar.copy(
-                out=e_grp[:], in_=live["eT", t][:].rearrange("p (g u) m -> p g m u", g=KEY_PASSES)
+                out=e_grp[:], in_=live["eT", t][:].rearrange("p (g j) m -> p g m j", g=KEY_PASSES)
             )
             live["e_grp", t] = e_grp
 
@@ -281,7 +302,7 @@ def tile_mvpam_module_mask_cascade_pb_kernel(tc, x, out1, q, k, wv2, bv2, gamma,
             nc.vector.quantize_mx(
                 out=e_codes[:].rearrange("p g m -> p (g m)").bitcast(FP8X4),
                 scales=e_scales[:].rearrange("p g m -> p (g m)"),
-                in_=live["e_grp", t][:].rearrange("p g m u -> p (g m u)"),
+                in_=live["e_grp", t][:].rearrange("p g m j -> p (g m j)").bitcast(BF16),
             )
             live["e_codes", t] = e_codes
             live["e_scales", t] = e_scales
@@ -361,16 +382,6 @@ def tile_mvpam_module_mask_cascade_pb_kernel(tc, x, out1, q, k, wv2, bv2, gamma,
         exponentials(1)
         regroup_out1(1, 0, nc.scalar.copy)
         regroup_out1(1, 1, nc.scalar.copy)
-
-        def values_half(b, g):
-            quantise_out1(b, g)
-            for piece in range(g * C_TILES, (g + 1) * C_TILES):
-                values_matmul(b, piece)
-                values_add_bias(b, piece)
-                if piece > g * C_TILES:
-                    values_quantise(b, piece - 1)
-            values_quantise(b, (g + 1) * C_TILES - 1)
-
         values_half(0, 0)
         turn_e(0)
         values_half(0, 1)
@@ -381,7 +392,7 @@ def tile_mvpam_module_mask_cascade_pb_kernel(tc, x, out1, q, k, wv2, bv2, gamma,
         quantise_out1(1, 0)
         row_max(2)
 
-        for r in range(2, TILES + LAG + 2):
+        for r in range(FIRST_ROUND, TILES + LAG + 2):
             back = r - LAG
             piece = r - PIECE_LEAD
             scores(r + 1)

@@ -239,7 +239,7 @@ def tile_mvpam_module_mask_cascade_pb_kernel(tc, x, out1, q, k, wv2, bv2, gamma,
                     out=bank_max[:, h : h + 1], in_=live["s", t][:, h, :], axis=AXIS_X, op=ALU.max
                 )
             neg_max = work.tile([P, 1], F32)
-            nc.vector.tensor_scalar(
+            nc.gpsimd.tensor_scalar(
                 out=neg_max[:],
                 in0=bank_max[:, 0:1],
                 scalar1=bank_max[:, 1:2],
@@ -263,8 +263,12 @@ def tile_mvpam_module_mask_cascade_pb_kernel(tc, x, out1, q, k, wv2, bv2, gamma,
                     scale=1.0,
                     accum_out=bank_sum[:, h : h + 1],
                 )
+            row_sum = work.tile([P, 1], F32)
+            nc.gpsimd.tensor_tensor(
+                out=row_sum[:], in0=bank_sum[:, 0:1], in1=bank_sum[:, 1:2], op=ALU.add
+            )
             live["e", t] = e_sb
-            live["bank_sum", t] = bank_sum
+            live["row_sum", t] = row_sum
 
         def turn_e(t):
             if not 0 <= t < TILES:
@@ -287,15 +291,8 @@ def tile_mvpam_module_mask_cascade_pb_kernel(tc, x, out1, q, k, wv2, bv2, gamma,
         def quantise_e(t):
             if not 0 <= t < TILES:
                 return
-            row_sum = work.tile([P, 1], F32)
-            nc.vector.tensor_tensor(
-                out=row_sum[:],
-                in0=live["bank_sum", t][:, 0:1],
-                in1=live["bank_sum", t][:, 1:2],
-                op=ALU.add,
-            )
             inv_sum = work.tile([P, 1], F32)
-            nc.vector.reciprocal(out=inv_sum[:], in_=row_sum[:])
+            nc.vector.reciprocal(out=inv_sum[:], in_=live["row_sum", t][:])
             live["inv_sum", t] = inv_sum
             e_codes = work.tile([P, KEY_PASSES, P], U32, align_bytes=64)
             e_scales = work.tile([P, KEY_PASSES, P], U8, align_bytes=64)

@@ -26,10 +26,8 @@ KEY_PASSES = N // K_PASS
 KEY_BANKS = N // BANK
 PIECES = KEY_PASSES * C_TILES
 STORE_TILES = 2
-FIRST_ROUND = 2
-LAG = 3
-PIECE_LEAD = FIRST_ROUND
-
+HEAD_TILES = 2
+VALUE_ROUNDS = 4
 FLOPS = 2 * B * (C * C * N + N * D * N + C * N * N)
 
 
@@ -39,44 +37,57 @@ def tile_mvpam_module_mask_cascade_pb_kernel(tc, x, out1, q, k, wv2, bv2, gamma,
         ctx.enter_context(tc.manual_schedule())
         const = ctx.enter_context(tc.tile_pool(name="const", bufs=1))
         per_batch = ctx.enter_context(tc.tile_pool(name="per_batch", bufs=B))
-        work = ctx.enter_context(tc.tile_pool(name="work", bufs=4))
+        work = ctx.enter_context(tc.tile_pool(name="work", bufs=6))
         ps_scores = ctx.enter_context(tc.psum_pool(name="ps_scores", bufs=2))
         ps_turn = ctx.enter_context(tc.psum_pool(name="ps_turn", bufs=2))
         ps_mx = ctx.enter_context(tc.psum_pool(name="ps_mx", bufs=2))
 
         q_sb, k_sb, o1_sb, x_sb = [], [], [], []
 
-        def load_scores_inputs(b):
-            q_rows = per_batch.tile([P, M_TILES, D], BF16)
-            nc.sync.dma_start(out=q_rows[:], in_=q[b].rearrange("(i p) d -> p i d", p=P))
-            q_sb.append(q_rows)
+        def load_queries(b, first, last):
+            if first == 0:
+                q_rows = per_batch.tile([P, M_TILES, D], BF16)
+                q_sb.append(q_rows)
+            nc.sync.dma_start(
+                out=q_sb[b][:, first:last, :], in_=q[b].rearrange("(i p) d -> p i d", p=P)[:, first:last, :]
+            )
+
+        def load_keys(b):
             k_rows = per_batch.tile([P, N], BF16)
             nc.sync.dma_start(out=k_rows[:], in_=k[b])
             k_sb.append(k_rows)
 
-        def load_out1(b):
-            o1_rows = per_batch.tile([P, PACK, N], BF16)
-            nc.sync.dma_start(
-                out=o1_rows[:].rearrange("p (j e) n -> p j e n", e=PAIR),
-                in_=out1[b].rearrange("(j p e) n -> p j e n", p=P, e=PAIR),
-            )
-            o1_sb.append(o1_rows)
+        def load_out1(b, g):
+            if g == 0:
+                o1_rows = per_batch.tile([P, PACK, N], BF16)
+                o1_sb.append(o1_rows)
+            keys = slice(g * K_PASS, (g + 1) * K_PASS)
+            for j in range(HALVES):
+                nc.sync.dma_start(
+                    out=o1_sb[b][:, j * PAIR : (j + 1) * PAIR, keys],
+                    in_=out1[b].rearrange("(j p e) n -> j p e n", p=P, e=PAIR)[j, :, :, keys],
+                )
 
         def load_x(b):
             x_rows = per_batch.tile([P, C_TILES, N], BF16)
             nc.sync.dma_start(out=x_rows[:], in_=x[b].rearrange("(ct p) m -> p ct m", p=P))
             x_sb.append(x_rows)
 
-        load_scores_inputs(0)
+        load_queries(0, 0, HEAD_TILES)
+        load_keys(0)
         w_sb = const.tile([P, C_TILES, C], BF16)
         nc.sync.dma_start(out=w_sb[:], in_=wv2.rearrange("(ct p) ci -> p ct ci", p=P))
-        load_out1(0)
+        load_out1(0, 0)
+        load_queries(0, HEAD_TILES, M_TILES)
         bias_bc = const.tile([P, C], BF16)
         nc.sync.dma_start(out=bias_bc[:], in_=bv2.partition_broadcast(P))
+        load_out1(0, 1)
         gamma_bf = const.tile([P, 1], BF16)
         nc.sync.dma_start(out=gamma_bf[:], in_=gamma.partition_broadcast(P))
-        load_scores_inputs(1)
-        load_out1(1)
+        load_out1(1, 0)
+        load_queries(1, 0, M_TILES)
+        load_keys(1)
+        load_out1(1, 1)
         load_x(0)
         load_x(1)
 
@@ -91,13 +102,17 @@ def tile_mvpam_module_mask_cascade_pb_kernel(tc, x, out1, q, k, wv2, bv2, gamma,
 
         qT_sb = []
 
-        def turn_queries(b):
+        def turn_queries(b, first, last):
+            if first == 0:
+                qT = per_batch.tile([P, N], BF16)
+                qT_sb.append(qT)
             qT_ps = ps_turn.tile([P, M_TILES, P], BF16, tag="turn")
-            for i in range(M_TILES):
+            for i in range(first, last):
                 nc.tensor.transpose(qT_ps[:, i, :], q_sb[b][:, i, :], ident_bf[:])
-            qT = per_batch.tile([P, N], BF16)
-            nc.scalar.copy(out=qT[:], in_=qT_ps[:].rearrange("d i m -> d (i m)"))
-            qT_sb.append(qT)
+            nc.scalar.copy(
+                out=qT_sb[b][:, first * P : last * P],
+                in_=qT_ps[:, first:last, :].rearrange("d i m -> d (i m)"),
+            )
 
         w_grp = const.tile([P, C, HALVES], F32, align_bytes=64)
         w_codes = const.tile([P, C], U32, align_bytes=64)
@@ -147,13 +162,17 @@ def tile_mvpam_module_mask_cascade_pb_kernel(tc, x, out1, q, k, wv2, bv2, gamma,
             )
         vT_banks = {}
 
-        def regroup_out1(b, g, copy):
-            for j in range(HALVES):
-                keys = slice(g * K_PASS + j * PAIR * P, g * K_PASS + (j + 1) * PAIR * P)
-                copy(
-                    out=values[b]["o1_grp"][:, keys, :].rearrange("p (e q) u -> p e q u", e=PAIR),
-                    in_=o1_sb[b][:, :, keys].rearrange("p u (q e) -> p e q u", e=PAIR),
-                )
+        def regroup_out1(b, g, j, e, copy):
+            keys = slice(g * K_PASS + j * PAIR * P, g * K_PASS + (j + 1) * PAIR * P)
+            copy(
+                out=values[b]["o1_grp"][:, keys, :].rearrange("p (e q) u -> p e q u", e=PAIR)[:, e],
+                in_=o1_sb[b][:, :, keys].rearrange("p u (q e) -> p e q u", e=PAIR)[:, e],
+            )
+
+        def gpsimd_copy(out, in_):
+            nc.gpsimd.tensor_scalar(
+                out=out, in0=in_, scalar1=1.0, scalar2=0.0, op0=ALU.mult, op1=ALU.add
+            )
 
         def quantise_out1(b, g):
             keys = slice(g * K_PASS, (g + 1) * K_PASS)
@@ -205,13 +224,6 @@ def tile_mvpam_module_mask_cascade_pb_kernel(tc, x, out1, q, k, wv2, bv2, gamma,
                 scales=values[b]["v_scales"][:, g, :],
                 in_=values[b]["v_grp"][:, g, :, :].rearrange("p c u -> p (c u)"),
             )
-
-        def values_half(b, g):
-            quantise_out1(b, g)
-            for piece in range(g * C_TILES, (g + 1) * C_TILES):
-                values_matmul(b, piece)
-                values_add_bias(b, piece)
-                values_quantise(b, piece)
 
         live = {}
 
@@ -291,9 +303,6 @@ def tile_mvpam_module_mask_cascade_pb_kernel(tc, x, out1, q, k, wv2, bv2, gamma,
         def quantise_e(t):
             if not 0 <= t < TILES:
                 return
-            inv_sum = work.tile([P, 1], F32)
-            nc.vector.reciprocal(out=inv_sum[:], in_=live["row_sum", t][:])
-            live["inv_sum", t] = inv_sum
             e_codes = work.tile([P, KEY_PASSES, P], U32, align_bytes=64)
             e_scales = work.tile([P, KEY_PASSES, P], U8, align_bytes=64)
             nc.vector.quantize_mx(
@@ -304,41 +313,59 @@ def tile_mvpam_module_mask_cascade_pb_kernel(tc, x, out1, q, k, wv2, bv2, gamma,
             live["e_codes", t] = e_codes
             live["e_scales", t] = e_scales
 
+        def invert_sum(t):
+            if not 0 <= t < TILES:
+                return
+            inv_sum = work.tile([P, 1], F32)
+            nc.vector.reciprocal(out=inv_sum[:], in_=live["row_sum", t][:])
+            live["inv_sum", t] = inv_sum
+
+        def spread_inverse(t):
+            if not 0 <= t < TILES:
+                return
+            inv_ps = ps_turn.tile([P, P], F32, tag="turn")
+            nc.tensor.transpose(inv_ps[:], live["inv_sum", t][:].to_broadcast([P, P]), ident_f32[:])
+            live["inv_ps", t] = inv_ps
+
+        def scale_inverse(t):
+            if not 0 <= t < TILES:
+                return
+            inv_bc = work.tile([P, P], F32)
+            nc.scalar.activation(
+                out=inv_bc[:], in_=live["inv_ps", t][:], func=ACT.Copy, scale=gamma_f32[:]
+            )
+            live["inv_bc", t] = inv_bc
+
         def attend(t):
             if not 0 <= t < TILES:
                 return
             b = t // M_TILES
-            attT_ps = ps_mx.tile([P, C], F32, tag="mx")
-            for g in range(KEY_PASSES):
-                nc.tensor.matmul_mx(
-                    out=attT_ps[:],
-                    lhsT=live["e_codes", t][:, g, :].bitcast(FP8X4),
-                    lhsT_scale=live["e_scales", t][:, g, :],
-                    rhs=values[b]["v_codes"][:, g, :].bitcast(FP8X4),
-                    rhs_scale=values[b]["v_scales"][:, g, :],
-                    start=(g == 0),
-                    stop=(g == KEY_PASSES - 1),
-                )
-            live["attT_ps", t] = attT_ps
-
-        def normalise(t):
-            if not 0 <= t < TILES:
-                return
-            attT_sb = work.tile([P, C], F32)
-            nc.scalar.activation(
-                out=attT_sb[:], in_=live["attT_ps", t][:], func=ACT.Copy, scale=live["inv_sum", t][:]
-            )
-            live["attT_sb", t] = attT_sb
-
-        def turn_att(t):
-            if not 0 <= t < TILES:
-                return
-            att_ps = ps_turn.tile([P, C_TILES, P], F32, tag="turn")
+            att_ps = ps_mx.tile([P, C_TILES, P], F32, tag="mx")
             for ct in range(C_TILES):
-                nc.tensor.transpose(
-                    att_ps[:, ct, :], live["attT_sb", t][:, ct * P : (ct + 1) * P], ident_f32[:]
-                )
+                chans = slice(ct * P, (ct + 1) * P)
+                for g in range(KEY_PASSES):
+                    nc.tensor.matmul_mx(
+                        out=att_ps[:, ct, :],
+                        lhsT=values[b]["v_codes"][:, g, chans].bitcast(FP8X4),
+                        lhsT_scale=values[b]["v_scales"][:, g, chans],
+                        rhs=live["e_codes", t][:, g, :].bitcast(FP8X4),
+                        rhs_scale=live["e_scales", t][:, g, :],
+                        start=(g == 0),
+                        stop=(g == KEY_PASSES - 1),
+                    )
             live["att", t] = att_ps
+
+        def divide(t):
+            if not 0 <= t < TILES:
+                return
+            att_sb = work.tile([P, C_TILES, P], F32)
+            nc.vector.tensor_tensor(
+                out=att_sb[:],
+                in0=live["att", t][:],
+                in1=live["inv_bc", t][:].unsqueeze(1).to_broadcast([P, C_TILES, P]),
+                op=ALU.mult,
+            )
+            live["att_sb", t] = att_sb
 
         def finish(t):
             if not 0 <= t < TILES:
@@ -349,13 +376,12 @@ def tile_mvpam_module_mask_cascade_pb_kernel(tc, x, out1, q, k, wv2, bv2, gamma,
                 out_sb = work.tile([P, C_TILES, STORE_TILES * P], F32)
                 live["out", t // STORE_TILES] = out_sb
             out_sb = live["out", t // STORE_TILES]
-            nc.vector.scalar_tensor_tensor(
+            eng = nc.vector if t >= TILES - 2 else nc.gpsimd
+            eng.tensor_tensor(
                 out=out_sb[:, :, part * P : (part + 1) * P],
-                in0=live["att", t][:],
-                scalar=gamma_f32[:],
+                in0=live["att_sb", t][:],
                 in1=x_sb[b][:, :, i * P : (i + 1) * P],
-                op0=ALU.mult,
-                op1=ALU.add,
+                op=ALU.add,
             )
             if part == STORE_TILES - 1:
                 first = (i - part) * P
@@ -364,46 +390,70 @@ def tile_mvpam_module_mask_cascade_pb_kernel(tc, x, out1, q, k, wv2, bv2, gamma,
                     in_=out_sb[:],
                 )
 
-        turn_queries(0)
+        all_e = slice(0, PAIR)
+        turn_queries(0, 0, HEAD_TILES)
         scores(0)
         row_max(0)
         scores(1)
         row_max(1)
         turn_weights()
-        regroup_out1(0, 0, nc.vector.tensor_copy)
-        regroup_out1(0, 1, nc.scalar.copy)
+        turn_queries(0, HEAD_TILES, M_TILES)
+        for j in range(HALVES):
+            regroup_out1(0, 0, j, all_e, nc.vector.tensor_copy)
+        for j in range(HALVES):
+            for e in range(PAIR):
+                regroup_out1(0, 1, j, slice(e, e + 1), gpsimd_copy)
         quantise_weights()
+        quantise_out1(0, 0)
         gamma_f32 = const.tile([P, 1], F32)
         nc.vector.tensor_copy(out=gamma_f32[:], in_=gamma_bf[:])
-        exponentials(0)
-        exponentials(1)
-        regroup_out1(1, 0, nc.scalar.copy)
-        regroup_out1(1, 1, nc.scalar.copy)
-        values_half(0, 0)
-        turn_e(0)
-        values_half(0, 1)
-        turn_queries(1)
-        scores(2)
-        group_e(0)
-        turn_e(1)
-        quantise_out1(1, 0)
-        row_max(2)
 
-        for r in range(FIRST_ROUND, TILES + LAG + 2):
-            back = r - LAG
-            piece = r - PIECE_LEAD
-            scores(r + 1)
+        attended = 0
+        divided = 0
+        before = []
+        for r in range(TILES + HEAD_TILES + 1):
+            pieces = []
+            now = []
+            if r < VALUE_ROUNDS:
+                pieces = [(0, 2 * r), (0, 2 * r + 1)]
+            elif r - VALUE_ROUNDS < PIECES:
+                pieces = [(1, r - VALUE_ROUNDS)]
+            if r >= VALUE_ROUNDS:
+                if r + HEAD_TILES < TILES:
+                    now = [attended]
+                else:
+                    now = [t for t in (attended, attended + 1) if t <= min(r - 2, TILES - 1)]
             exponentials(r)
-            finish(back - 2)
-            values_add_bias(1, piece - 1)
-            attend(back)
-            values_matmul(1, piece)
-            turn_att(back - 1)
+            scores(r + HEAD_TILES)
+            if r == 2:
+                turn_queries(1, 0, M_TILES)
             group_e(r - 1)
-            turn_e(r)
-            normalise(back)
+            scale_inverse(r - 3)
             quantise_e(r - 2)
-            values_quantise(1, piece - 1)
-            if piece + 1 == C_TILES:
+            for b, piece in before:
+                values_quantise(b, piece)
+            invert_sum(r - 1)
+            spread_inverse(r - 2)
+            turn_e(r)
+            for t in range(divided, attended):
+                divide(t)
+                finish(t)
+            divided = attended
+            attended += len(now)
+            row_max(r + HEAD_TILES)
+            if r == 1:
+                quantise_out1(0, 1)
+            if r == 3:
+                quantise_out1(1, 0)
+            if r == 6:
                 quantise_out1(1, 1)
-            row_max(r + 1)
+            for b, piece in pieces:
+                values_matmul(b, piece)
+                values_add_bias(b, piece)
+            before = pieces
+            for t in now:
+                attend(t)
+            if 1 <= r <= 4:
+                g, j = divmod(r - 1, HALVES)
+                for e in range(PAIR):
+                    regroup_out1(1, g, j, slice(e, e + 1), gpsimd_copy)

@@ -37,12 +37,14 @@ def tile_mvpam_module_mask_cascade_pb_kernel(tc, x, out1, q, k, wv2, bv2, gamma,
         ctx.enter_context(tc.manual_schedule())
         const = ctx.enter_context(tc.tile_pool(name="const", bufs=1))
         per_batch = ctx.enter_context(tc.tile_pool(name="per_batch", bufs=B))
+        halves = ctx.enter_context(tc.tile_pool(name="halves", bufs=B * KEY_PASSES))
         work = ctx.enter_context(tc.tile_pool(name="work", bufs=6))
         ps_scores = ctx.enter_context(tc.psum_pool(name="ps_scores", bufs=2))
         ps_turn = ctx.enter_context(tc.psum_pool(name="ps_turn", bufs=2))
         ps_mx = ctx.enter_context(tc.psum_pool(name="ps_mx", bufs=2))
 
-        q_sb, k_sb, o1_sb, x_sb = [], [], [], []
+        q_sb, k_sb, x_sb = [], [], []
+        o1_sb = {}
 
         def load_queries(b, first, last):
             if first == 0:
@@ -58,13 +60,12 @@ def tile_mvpam_module_mask_cascade_pb_kernel(tc, x, out1, q, k, wv2, bv2, gamma,
             k_sb.append(k_rows)
 
         def load_out1(b, g):
-            if g == 0:
-                o1_rows = per_batch.tile([P, PACK, N], BF16)
-                o1_sb.append(o1_rows)
+            o1_rows = halves.tile([P, PACK, K_PASS], BF16)
+            o1_sb[b, g] = o1_rows
             keys = slice(g * K_PASS, (g + 1) * K_PASS)
             for j in range(HALVES):
                 nc.sync.dma_start(
-                    out=o1_sb[b][:, j * PAIR : (j + 1) * PAIR, keys],
+                    out=o1_rows[:, j * PAIR : (j + 1) * PAIR, :],
                     in_=out1[b].rearrange("(j p e) n -> j p e n", p=P, e=PAIR)[j, :, :, keys],
                 )
 
@@ -74,14 +75,14 @@ def tile_mvpam_module_mask_cascade_pb_kernel(tc, x, out1, q, k, wv2, bv2, gamma,
             x_sb.append(x_rows)
 
         load_queries(0, 0, HEAD_TILES)
+        load_out1(0, 0)
         load_keys(0)
+        load_queries(0, HEAD_TILES, M_TILES)
         w_sb = const.tile([P, C_TILES, C], BF16)
         nc.sync.dma_start(out=w_sb[:], in_=wv2.rearrange("(ct p) ci -> p ct ci", p=P))
-        load_out1(0, 0)
-        load_queries(0, HEAD_TILES, M_TILES)
         bias_bc = const.tile([P, C], BF16)
-        nc.sync.dma_start(out=bias_bc[:], in_=bv2.partition_broadcast(P))
         load_out1(0, 1)
+        nc.sync.dma_start(out=bias_bc[:], in_=bv2.partition_broadcast(P))
         gamma_bf = const.tile([P, 1], BF16)
         nc.sync.dma_start(out=gamma_bf[:], in_=gamma.partition_broadcast(P))
         load_out1(1, 0)
@@ -118,7 +119,7 @@ def tile_mvpam_module_mask_cascade_pb_kernel(tc, x, out1, q, k, wv2, bv2, gamma,
         w_codes = const.tile([P, C], U32, align_bytes=64)
         w_scales = const.tile([P, C], U8, align_bytes=64)
 
-        def turn_weights():
+        def turn_weights(copy):
             per_bank = BANK // (HALVES * P)
             for first in range(0, C_TILES, per_bank):
                 wT_ps = ps_turn.tile([P, per_bank, HALVES, P], F32, tag="turn")
@@ -128,7 +129,7 @@ def tile_mvpam_module_mask_cascade_pb_kernel(tc, x, out1, q, k, wv2, bv2, gamma,
                         nc.tensor.transpose(
                             wT_ps[:, a, j, :], w_words[:, j * P : (j + 1) * P], ident_f32[:]
                         )
-                nc.scalar.copy(
+                copy(
                     out=w_grp[:, first * P : (first + per_bank) * P, :].rearrange(
                         "p (a c) j -> p a c j", a=per_bank
                     ),
@@ -166,7 +167,7 @@ def tile_mvpam_module_mask_cascade_pb_kernel(tc, x, out1, q, k, wv2, bv2, gamma,
             keys = slice(g * K_PASS + j * PAIR * P, g * K_PASS + (j + 1) * PAIR * P)
             copy(
                 out=values[b]["o1_grp"][:, keys, :].rearrange("p (e q) u -> p e q u", e=PAIR)[:, e],
-                in_=o1_sb[b][:, :, keys].rearrange("p u (q e) -> p e q u", e=PAIR)[:, e],
+                in_=o1_sb[b, g][:, :, j * PAIR * P : (j + 1) * PAIR * P].rearrange("p u (q e) -> p e q u", e=PAIR)[:, e],
             )
 
         def gpsimd_copy(out, in_):
@@ -391,20 +392,20 @@ def tile_mvpam_module_mask_cascade_pb_kernel(tc, x, out1, q, k, wv2, bv2, gamma,
                 )
 
         all_e = slice(0, PAIR)
+        for j in range(HALVES):
+            regroup_out1(0, 0, j, all_e, nc.vector.tensor_copy)
         turn_queries(0, 0, HEAD_TILES)
         scores(0)
         row_max(0)
         scores(1)
         row_max(1)
-        turn_weights()
         turn_queries(0, HEAD_TILES, M_TILES)
-        for j in range(HALVES):
-            regroup_out1(0, 0, j, all_e, nc.vector.tensor_copy)
+        quantise_out1(0, 0)
+        turn_weights(nc.vector.tensor_copy)
         for j in range(HALVES):
             for e in range(PAIR):
                 regroup_out1(0, 1, j, slice(e, e + 1), gpsimd_copy)
         quantise_weights()
-        quantise_out1(0, 0)
         gamma_f32 = const.tile([P, 1], F32)
         nc.vector.tensor_copy(out=gamma_f32[:], in_=gamma_bf[:])
 
@@ -418,42 +419,43 @@ def tile_mvpam_module_mask_cascade_pb_kernel(tc, x, out1, q, k, wv2, bv2, gamma,
                 pieces = [(0, 2 * r), (0, 2 * r + 1)]
             elif r - VALUE_ROUNDS < PIECES:
                 pieces = [(1, r - VALUE_ROUNDS)]
-            if r >= VALUE_ROUNDS:
+            if r > VALUE_ROUNDS:
                 if r + HEAD_TILES < TILES:
                     now = [attended]
                 else:
                     now = [t for t in (attended, attended + 1) if t <= min(r - 2, TILES - 1)]
+            quantise_e(r - 1)
+            invert_sum(r - 1)
+            spread_inverse(r - 2)
             exponentials(r)
+            scale_inverse(r - 2)
+            turn_e(r)
+            group_e(r)
             scores(r + HEAD_TILES)
             if r == 2:
                 turn_queries(1, 0, M_TILES)
-            group_e(r - 1)
-            scale_inverse(r - 3)
-            quantise_e(r - 2)
-            for b, piece in before:
-                values_quantise(b, piece)
-            invert_sum(r - 1)
-            spread_inverse(r - 2)
-            turn_e(r)
             for t in range(divided, attended):
                 divide(t)
                 finish(t)
             divided = attended
             attended += len(now)
+            for b, piece in before:
+                values_add_bias(b, piece)
             row_max(r + HEAD_TILES)
-            if r == 1:
+            for b, piece in before:
+                values_quantise(b, piece)
+            for t in now:
+                attend(t)
+            for b, piece in pieces:
+                values_matmul(b, piece)
+            before = pieces
+            if 0 < r <= VALUE_ROUNDS:
+                g, j = divmod(r - 1, HALVES)
+                for e in range(PAIR):
+                    regroup_out1(1, g, j, slice(e, e + 1), gpsimd_copy)
+            if r == 0:
                 quantise_out1(0, 1)
             if r == 3:
                 quantise_out1(1, 0)
             if r == 6:
                 quantise_out1(1, 1)
-            for b, piece in pieces:
-                values_matmul(b, piece)
-                values_add_bias(b, piece)
-            before = pieces
-            for t in now:
-                attend(t)
-            if 1 <= r <= 4:
-                g, j = divmod(r - 1, HALVES)
-                for e in range(PAIR):
-                    regroup_out1(1, g, j, slice(e, e + 1), gpsimd_copy)

@@ -321,52 +321,41 @@ def tile_mvpam_module_mask_cascade_pb_kernel(tc, x, out1, q, k, wv2, bv2, gamma,
             nc.vector.reciprocal(out=inv_sum[:], in_=live["row_sum", t][:])
             live["inv_sum", t] = inv_sum
 
-        def spread_inverse(t):
-            if not 0 <= t < TILES:
-                return
-            inv_ps = ps_turn.tile([P, P], F32, tag="turn")
-            nc.tensor.transpose(inv_ps[:], live["inv_sum", t][:].to_broadcast([P, P]), ident_f32[:])
-            live["inv_ps", t] = inv_ps
-
-        def scale_inverse(t):
-            if not 0 <= t < TILES:
-                return
-            inv_bc = work.tile([P, P], F32)
-            nc.scalar.activation(
-                out=inv_bc[:], in_=live["inv_ps", t][:], func=ACT.Copy, scale=gamma_f32[:]
-            )
-            live["inv_bc", t] = inv_bc
-
         def attend(t):
             if not 0 <= t < TILES:
                 return
             b = t // M_TILES
-            att_ps = ps_mx.tile([P, C_TILES, P], F32, tag="mx")
-            for ct in range(C_TILES):
-                chans = slice(ct * P, (ct + 1) * P)
-                for g in range(KEY_PASSES):
-                    nc.tensor.matmul_mx(
-                        out=att_ps[:, ct, :],
-                        lhsT=values[b]["v_codes"][:, g, chans].bitcast(FP8X4),
-                        lhsT_scale=values[b]["v_scales"][:, g, chans],
-                        rhs=live["e_codes", t][:, g, :].bitcast(FP8X4),
-                        rhs_scale=live["e_scales", t][:, g, :],
-                        start=(g == 0),
-                        stop=(g == KEY_PASSES - 1),
-                    )
-            live["att", t] = att_ps
+            attT_ps = ps_mx.tile([P, C], F32, tag="mx")
+            for g in range(KEY_PASSES):
+                nc.tensor.matmul_mx(
+                    out=attT_ps[:],
+                    lhsT=live["e_codes", t][:, g, :].bitcast(FP8X4),
+                    lhsT_scale=live["e_scales", t][:, g, :],
+                    rhs=values[b]["v_codes"][:, g, :].bitcast(FP8X4),
+                    rhs_scale=values[b]["v_scales"][:, g, :],
+                    start=(g == 0),
+                    stop=(g == KEY_PASSES - 1),
+                )
+            live["attT_ps", t] = attT_ps
 
-        def divide(t):
+        def normalise(t):
             if not 0 <= t < TILES:
                 return
-            att_sb = work.tile([P, C_TILES, P], F32)
-            nc.vector.tensor_tensor(
-                out=att_sb[:],
-                in0=live["att", t][:],
-                in1=live["inv_bc", t][:].unsqueeze(1).to_broadcast([P, C_TILES, P]),
-                op=ALU.mult,
+            attT_sb = work.tile([P, C], F32)
+            nc.scalar.activation(
+                out=attT_sb[:], in_=live["attT_ps", t][:], func=ACT.Copy, scale=live["inv_sum", t][:]
             )
-            live["att_sb", t] = att_sb
+            live["attT_sb", t] = attT_sb
+
+        def turn_att(t):
+            if not 0 <= t < TILES:
+                return
+            att_ps = ps_turn.tile([P, C_TILES, P], F32, tag="turn")
+            for ct in range(C_TILES):
+                nc.tensor.transpose(
+                    att_ps[:, ct, :], live["attT_sb", t][:, ct * P : (ct + 1) * P], ident_f32[:]
+                )
+            live["att", t] = att_ps
 
         def finish(t):
             if not 0 <= t < TILES:
@@ -377,12 +366,13 @@ def tile_mvpam_module_mask_cascade_pb_kernel(tc, x, out1, q, k, wv2, bv2, gamma,
                 out_sb = work.tile([P, C_TILES, STORE_TILES * P], F32)
                 live["out", t // STORE_TILES] = out_sb
             out_sb = live["out", t // STORE_TILES]
-            eng = nc.vector if t >= TILES - 2 else nc.gpsimd
-            eng.tensor_tensor(
+            nc.vector.scalar_tensor_tensor(
                 out=out_sb[:, :, part * P : (part + 1) * P],
-                in0=live["att_sb", t][:],
+                in0=live["att", t][:],
+                scalar=gamma_f32[:],
                 in1=x_sb[b][:, :, i * P : (i + 1) * P],
-                op=ALU.add,
+                op0=ALU.mult,
+                op1=ALU.add,
             )
             if part == STORE_TILES - 1:
                 first = (i - part) * P
@@ -410,35 +400,37 @@ def tile_mvpam_module_mask_cascade_pb_kernel(tc, x, out1, q, k, wv2, bv2, gamma,
         nc.vector.tensor_copy(out=gamma_f32[:], in_=gamma_bf[:])
 
         attended = 0
-        divided = 0
+        scaled = 0
+        turned = 0
         before = []
-        for r in range(TILES + HEAD_TILES + 1):
+        for r in range(TILES + HEAD_TILES + 2):
             pieces = []
             now = []
             if r < VALUE_ROUNDS:
                 pieces = [(0, 2 * r), (0, 2 * r + 1)]
             elif r - VALUE_ROUNDS < PIECES:
                 pieces = [(1, r - VALUE_ROUNDS)]
-            if r > VALUE_ROUNDS:
+            if r > VALUE_ROUNDS + 0:
                 if r + HEAD_TILES < TILES:
                     now = [attended]
                 else:
-                    now = [t for t in (attended, attended + 1) if t <= min(r - 2, TILES - 1)]
+                    now = [t for t in range(attended, attended + 2) if t <= min(r - 2, TILES - 1)]
             quantise_e(r - 1)
             invert_sum(r - 1)
-            spread_inverse(r - 2)
             exponentials(r)
-            scale_inverse(r - 2)
+            for t in range(turned, scaled):
+                turn_att(t)
+                finish(t)
+            turned = scaled
+            for t in range(scaled, attended):
+                normalise(t)
+            scaled = attended
+            attended += len(now)
             turn_e(r)
             group_e(r)
             scores(r + HEAD_TILES)
             if r == 2:
                 turn_queries(1, 0, M_TILES)
-            for t in range(divided, attended):
-                divide(t)
-                finish(t)
-            divided = attended
-            attended += len(now)
             for b, piece in before:
                 values_add_bias(b, piece)
             row_max(r + HEAD_TILES)

@@ -26,6 +26,7 @@ KEY_PASSES = N // K_PASS
 KEY_BANKS = N // BANK
 PIECES = KEY_PASSES * C_TILES
 STORE_TILES = 2
+FIRST_Q = 2
 HEAD_TILES = 2
 VALUE_ROUNDS = 4
 FLOPS = 2 * B * (C * C * N + N * D * N + C * N * N)
@@ -74,14 +75,14 @@ def tile_mvpam_module_mask_cascade_pb_kernel(tc, x, out1, q, k, wv2, bv2, gamma,
             nc.sync.dma_start(out=x_rows[:], in_=x[b].rearrange("(ct p) m -> p ct m", p=P))
             x_sb.append(x_rows)
 
-        load_queries(0, 0, HEAD_TILES)
+        load_queries(0, 0, FIRST_Q)
         load_out1(0, 0)
         load_keys(0)
-        load_queries(0, HEAD_TILES, M_TILES)
+        load_queries(0, FIRST_Q, M_TILES)
         w_sb = const.tile([P, C_TILES, C], BF16)
         nc.sync.dma_start(out=w_sb[:], in_=wv2.rearrange("(ct p) ci -> p ct ci", p=P))
-        bias_bc = const.tile([P, C], BF16)
         load_out1(0, 1)
+        bias_bc = const.tile([P, C], BF16)
         nc.sync.dma_start(out=bias_bc[:], in_=bv2.partition_broadcast(P))
         gamma_bf = const.tile([P, 1], BF16)
         nc.sync.dma_start(out=gamma_bf[:], in_=gamma.partition_broadcast(P))
@@ -119,7 +120,7 @@ def tile_mvpam_module_mask_cascade_pb_kernel(tc, x, out1, q, k, wv2, bv2, gamma,
         w_codes = const.tile([P, C], U32, align_bytes=64)
         w_scales = const.tile([P, C], U8, align_bytes=64)
 
-        def turn_weights(copy):
+        def turn_weights(copies):
             per_bank = BANK // (HALVES * P)
             for first in range(0, C_TILES, per_bank):
                 wT_ps = ps_turn.tile([P, per_bank, HALVES, P], F32, tag="turn")
@@ -129,7 +130,7 @@ def tile_mvpam_module_mask_cascade_pb_kernel(tc, x, out1, q, k, wv2, bv2, gamma,
                         nc.tensor.transpose(
                             wT_ps[:, a, j, :], w_words[:, j * P : (j + 1) * P], ident_f32[:]
                         )
-                copy(
+                copies[first // per_bank](
                     out=w_grp[:, first * P : (first + per_bank) * P, :].rearrange(
                         "p (a c) j -> p a c j", a=per_bank
                     ),
@@ -232,7 +233,7 @@ def tile_mvpam_module_mask_cascade_pb_kernel(tc, x, out1, q, k, wv2, bv2, gamma,
             if not 0 <= t < TILES:
                 return
             b, i = divmod(t, M_TILES)
-            s_ps = ps_scores.tile([P, KEY_BANKS, BANK], F32)
+            s_ps = ps_scores.tile([P, KEY_BANKS, BANK], F32, tag="scores")
             for h in range(KEY_BANKS):
                 nc.tensor.matmul(
                     out=s_ps[:, h, :],
@@ -276,12 +277,16 @@ def tile_mvpam_module_mask_cascade_pb_kernel(tc, x, out1, q, k, wv2, bv2, gamma,
                     scale=1.0,
                     accum_out=bank_sum[:, h : h + 1],
                 )
-            row_sum = work.tile([P, 1], F32)
+            if t % 2 == 0:
+                row_sums = work.tile([P, 2], F32)
+                live["row_sums", t // 2] = row_sums
             nc.gpsimd.tensor_tensor(
-                out=row_sum[:], in0=bank_sum[:, 0:1], in1=bank_sum[:, 1:2], op=ALU.add
+                out=live["row_sums", t // 2][:, t % 2 : t % 2 + 1],
+                in0=bank_sum[:, 0:1],
+                in1=bank_sum[:, 1:2],
+                op=ALU.add,
             )
             live["e", t] = e_sb
-            live["row_sum", t] = row_sum
 
         def turn_e(t):
             if not 0 <= t < TILES:
@@ -317,18 +322,26 @@ def tile_mvpam_module_mask_cascade_pb_kernel(tc, x, out1, q, k, wv2, bv2, gamma,
         def invert_sum(t):
             if not 0 <= t < TILES:
                 return
-            inv_sum = work.tile([P, 1], F32)
-            nc.vector.reciprocal(out=inv_sum[:], in_=live["row_sum", t][:])
-            live["inv_sum", t] = inv_sum
+            if t % 2 == 0:
+                return
+            inv_sums = work.tile([P, 2], F32)
+            nc.vector.reciprocal(out=inv_sums[:], in_=live["row_sums", t // 2][:])
+            for n in range(2):
+                live["inv_sum", t - 1 + n] = inv_sums[:, n : n + 1]
 
         def attend(t):
             if not 0 <= t < TILES:
                 return
             b = t // M_TILES
-            attT_ps = ps_mx.tile([P, C], F32, tag="mx")
+            if t >= 11 and t % 2 == 1:
+                s_ps = ps_scores.tile([P, KEY_BANKS, BANK], F32, tag="scores")
+                attT_ps = s_ps[:, 0, :]
+            else:
+                mx_ps = ps_mx.tile([P, C], F32, tag="mx")
+                attT_ps = mx_ps[:]
             for g in range(KEY_PASSES):
                 nc.tensor.matmul_mx(
-                    out=attT_ps[:],
+                    out=attT_ps,
                     lhsT=live["e_codes", t][:, g, :].bitcast(FP8X4),
                     lhsT_scale=live["e_scales", t][:, g, :],
                     rhs=values[b]["v_codes"][:, g, :].bitcast(FP8X4),
@@ -343,14 +356,19 @@ def tile_mvpam_module_mask_cascade_pb_kernel(tc, x, out1, q, k, wv2, bv2, gamma,
                 return
             attT_sb = work.tile([P, C], F32)
             nc.scalar.activation(
-                out=attT_sb[:], in_=live["attT_ps", t][:], func=ACT.Copy, scale=live["inv_sum", t][:]
+                out=attT_sb[:], in_=live["attT_ps", t], func=ACT.Copy, scale=live["inv_sum", t]
             )
             live["attT_sb", t] = attT_sb
 
         def turn_att(t):
             if not 0 <= t < TILES:
                 return
-            att_ps = ps_turn.tile([P, C_TILES, P], F32, tag="turn")
+            if t >= 14:
+                s_ps = ps_scores.tile([P, KEY_BANKS, BANK], F32, tag="scores")
+                att_ps = s_ps[:, 0, :].rearrange("p (ct m) -> p ct m", ct=C_TILES)
+            else:
+                turn_ps = ps_turn.tile([P, C_TILES, P], F32, tag="turn")
+                att_ps = turn_ps[:]
             for ct in range(C_TILES):
                 nc.tensor.transpose(
                     att_ps[:, ct, :], live["attT_sb", t][:, ct * P : (ct + 1) * P], ident_f32[:]
@@ -368,53 +386,52 @@ def tile_mvpam_module_mask_cascade_pb_kernel(tc, x, out1, q, k, wv2, bv2, gamma,
             out_sb = live["out", t // STORE_TILES]
             nc.vector.scalar_tensor_tensor(
                 out=out_sb[:, :, part * P : (part + 1) * P],
-                in0=live["att", t][:],
-                scalar=gamma_f32[:],
+                in0=live["att", t],
+                scalar=gamma_bf[:],
                 in1=x_sb[b][:, :, i * P : (i + 1) * P],
                 op0=ALU.mult,
                 op1=ALU.add,
             )
-            if part == STORE_TILES - 1:
-                first = (i - part) * P
+            stored = 1 if t >= TILES - STORE_TILES else STORE_TILES
+            if (part + 1) % stored == 0:
+                cols = slice((part + 1 - stored) * P, (part + 1) * P)
+                first = (i + 1 - stored) * P
                 nc.sync.dma_start(
-                    out=out[b].rearrange("(ct p) m -> p ct m", p=P)[:, :, first : first + STORE_TILES * P],
-                    in_=out_sb[:],
+                    out=out[b].rearrange("(ct p) m -> p ct m", p=P)[:, :, first : first + stored * P],
+                    in_=out_sb[:, :, cols],
                 )
 
         all_e = slice(0, PAIR)
         for j in range(HALVES):
             regroup_out1(0, 0, j, all_e, nc.vector.tensor_copy)
-        turn_queries(0, 0, HEAD_TILES)
+        turn_queries(0, 0, FIRST_Q)
         scores(0)
         row_max(0)
         scores(1)
         row_max(1)
-        turn_queries(0, HEAD_TILES, M_TILES)
         quantise_out1(0, 0)
-        turn_weights(nc.vector.tensor_copy)
+        turn_queries(0, FIRST_Q, M_TILES)
+        turn_weights((nc.vector.tensor_copy, nc.vector.tensor_copy))
         for j in range(HALVES):
             for e in range(PAIR):
                 regroup_out1(0, 1, j, slice(e, e + 1), gpsimd_copy)
         quantise_weights()
-        gamma_f32 = const.tile([P, 1], F32)
-        nc.vector.tensor_copy(out=gamma_f32[:], in_=gamma_bf[:])
 
         attended = 0
         scaled = 0
         turned = 0
         before = []
-        for r in range(TILES + HEAD_TILES + 2):
+        done = 0
+        counts = [0,0,0,0,1,1,1,1,1,1,1,1]
+        atts = [0,0,0,0,0,1,1,1,1,1,1,1,1,1,2,2,2,1]
+        for r in range(TILES + HEAD_TILES + 3):
             pieces = []
-            now = []
             if r < VALUE_ROUNDS:
                 pieces = [(0, 2 * r), (0, 2 * r + 1)]
-            elif r - VALUE_ROUNDS < PIECES:
-                pieces = [(1, r - VALUE_ROUNDS)]
-            if r > VALUE_ROUNDS + 0:
-                if r + HEAD_TILES < TILES:
-                    now = [attended]
-                else:
-                    now = [t for t in range(attended, attended + 2) if t <= min(r - 2, TILES - 1)]
+            for n in range(counts[r] if r < len(counts) else 0):
+                pieces.append((1, done))
+                done += 1
+            now = [t for t in range(attended, attended + (atts[r] if r < len(atts) else 0))]
             quantise_e(r - 1)
             invert_sum(r - 1)
             exponentials(r)
@@ -441,7 +458,7 @@ def tile_mvpam_module_mask_cascade_pb_kernel(tc, x, out1, q, k, wv2, bv2, gamma,
             for b, piece in pieces:
                 values_matmul(b, piece)
             before = pieces
-            if 0 < r <= VALUE_ROUNDS:
+            if 1 <= r <= 4:
                 g, j = divmod(r - 1, HALVES)
                 for e in range(PAIR):
                     regroup_out1(1, g, j, slice(e, e + 1), gpsimd_copy)

@@ -432,8 +432,10 @@ def tile_mvpam_module_mask_cascade_pb_kernel(tc, x, out1, q, k, wv2, bv2, gamma,
                 pieces.append((1, done))
                 done += 1
             now = [t for t in range(attended, attended + (atts[r] if r < len(atts) else 0))]
-            quantise_e(r - 1)
-            invert_sum(r - 1)
+            in_time = r - 1 < TILES - HEAD_TILES - 1
+            if not in_time:
+                quantise_e(r - 1)
+                invert_sum(r - 1)
             exponentials(r)
             for t in range(turned, scaled):
                 turn_att(t)
@@ -450,6 +452,9 @@ def tile_mvpam_module_mask_cascade_pb_kernel(tc, x, out1, q, k, wv2, bv2, gamma,
                 turn_queries(1, 0, M_TILES)
             for b, piece in before:
                 values_add_bias(b, piece)
+            if in_time:
+                quantise_e(r - 1)
+                invert_sum(r - 1)
             row_max(r + HEAD_TILES)
             for b, piece in before:
                 values_quantise(b, piece)

@@ -437,9 +437,13 @@ def tile_mvpam_module_mask_cascade_pb_kernel(tc, x, out1, q, k, wv2, bv2, gamma,
                 quantise_e(r - 1)
                 invert_sum(r - 1)
             exponentials(r)
-            for t in range(turned, scaled):
+            if r == 2:
+                turn_queries(1, 0, M_TILES)
+            to_finish = range(turned, scaled)
+            for t in to_finish:
                 turn_att(t)
-                finish(t)
+                if not in_time:
+                    finish(t)
             turned = scaled
             for t in range(scaled, attended):
                 normalise(t)
@@ -448,14 +452,15 @@ def tile_mvpam_module_mask_cascade_pb_kernel(tc, x, out1, q, k, wv2, bv2, gamma,
             turn_e(r)
             group_e(r)
             scores(r + HEAD_TILES)
-            if r == 2:
-                turn_queries(1, 0, M_TILES)
             for b, piece in before:
                 values_add_bias(b, piece)
             if in_time:
+                for t in to_finish:
+                    finish(t)
+            row_max(r + HEAD_TILES)
+            if in_time:
                 quantise_e(r - 1)
                 invert_sum(r - 1)
-            row_max(r + HEAD_TILES)
             for b, piece in before:
                 values_quantise(b, piece)
             for t in now:

@@ -27,6 +27,10 @@ KEY_BANKS = N // BANK
 PIECES = KEY_PASSES * C_TILES
 STORE_TILES = 2
 FIRST_Q = 2
+FIRST_ATTEND = 5
+TURN_ROUND = 2
+E_LAG = 3
+LAST_OWED = TILES - 2
 HEAD_TILES = 2
 VALUE_ROUNDS = 4
 FLOPS = 2 * B * (C * C * N + N * D * N + C * N * N)
@@ -420,55 +424,57 @@ def tile_mvpam_module_mask_cascade_pb_kernel(tc, x, out1, q, k, wv2, bv2, gamma,
         attended = 0
         scaled = 0
         turned = 0
-        before = []
-        done = 0
-        counts = [0,0,0,0,1,1,1,1,1,1,1,1]
-        atts = [0,0,0,0,0,1,1,1,1,1,1,1,1,1,2,2,2,1]
-        for r in range(TILES + HEAD_TILES + 3):
-            pieces = []
+        quantised = 0
+        pieces_before = []
+        held = []
+        for r in range(TILES + HEAD_TILES + 2):
             if r < VALUE_ROUNDS:
                 pieces = [(0, 2 * r), (0, 2 * r + 1)]
-            for n in range(counts[r] if r < len(counts) else 0):
-                pieces.append((1, done))
-                done += 1
-            now = [t for t in range(attended, attended + (atts[r] if r < len(atts) else 0))]
-            in_time = r - 1 < TILES - HEAD_TILES - 1
-            if not in_time:
+            elif r - VALUE_ROUNDS < PIECES:
+                pieces = [(1, r - VALUE_ROUNDS)]
+            else:
+                pieces = []
+            at_once = 0 if r < FIRST_ATTEND else 1 if r + HEAD_TILES < TILES else 2
+            now = range(attended, min(attended + at_once, TILES))
+            to_scale = range(scaled, attended)
+            to_finish = range(turned, scaled)
+            turned, scaled, attended = scaled, attended, attended + len(now)
+
+            if r > LAST_OWED:
                 quantise_e(r - 1)
                 invert_sum(r - 1)
             exponentials(r)
-            if r == 2:
+            if r == TURN_ROUND:
                 turn_queries(1, 0, M_TILES)
-            to_finish = range(turned, scaled)
+            for b, piece in held:
+                values_matmul(b, piece)
             for t in to_finish:
                 turn_att(t)
-                if not in_time:
-                    finish(t)
-            turned = scaled
-            for t in range(scaled, attended):
+            for t in to_scale:
                 normalise(t)
-            scaled = attended
-            attended += len(now)
             turn_e(r)
             group_e(r)
             scores(r + HEAD_TILES)
-            for b, piece in before:
+            for b, piece in pieces_before:
                 values_add_bias(b, piece)
-            if in_time:
-                for t in to_finish:
-                    finish(t)
+            for t in to_finish:
+                finish(t)
             row_max(r + HEAD_TILES)
-            if in_time:
-                quantise_e(r - 1)
+            if r <= LAST_OWED:
+                for t in range(quantised, r if r == LAST_OWED else r - E_LAG + 1):
+                    quantise_e(t)
+                    quantised = t + 1
                 invert_sum(r - 1)
-            for b, piece in before:
+            for b, piece in pieces_before:
                 values_quantise(b, piece)
             for t in now:
                 attend(t)
-            for b, piece in pieces:
-                values_matmul(b, piece)
-            before = pieces
-            if 1 <= r <= 4:
+            held = pieces if r == TURN_ROUND - 1 else []
+            if not held:
+                for b, piece in pieces:
+                    values_matmul(b, piece)
+            pieces_before = pieces
+            if 1 <= r <= KEY_PASSES * HALVES:
                 g, j = divmod(r - 1, HALVES)
                 for e in range(PAIR):
                     regroup_out1(1, g, j, slice(e, e + 1), gpsimd_copy)

@@ -80,8 +80,8 @@ def tile_mvpam_module_mask_cascade_pb_kernel(tc, x, out1, q, k, wv2, bv2, gamma,
             x_sb.append(x_rows)
 
         load_queries(0, 0, FIRST_Q)
-        load_out1(0, 0)
         load_keys(0)
+        load_out1(0, 0)
         load_queries(0, FIRST_Q, M_TILES)
         w_sb = const.tile([P, C_TILES, C], BF16)
         nc.sync.dma_start(out=w_sb[:], in_=wv2.rearrange("(ct p) ci -> p ct ci", p=P))
@@ -406,12 +406,13 @@ def tile_mvpam_module_mask_cascade_pb_kernel(tc, x, out1, q, k, wv2, bv2, gamma,
                 )
 
         all_e = slice(0, PAIR)
-        for j in range(HALVES):
-            regroup_out1(0, 0, j, all_e, nc.vector.tensor_copy)
         turn_queries(0, 0, FIRST_Q)
         scores(0)
-        row_max(0)
         scores(1)
+        regroup_out1(0, 0, 0, all_e, nc.vector.tensor_copy)
+        for e in range(PAIR):
+            regroup_out1(0, 0, 1, slice(e, e + 1), nc.scalar.copy)
+        row_max(0)
         row_max(1)
         quantise_out1(0, 0)
         turn_queries(0, FIRST_Q, M_TILES)
@@ -448,11 +449,14 @@ def tile_mvpam_module_mask_cascade_pb_kernel(tc, x, out1, q, k, wv2, bv2, gamma,
                 turn_queries(1, 0, M_TILES)
             for b, piece in held:
                 values_matmul(b, piece)
+            if r <= LAST_OWED:
+                turn_e(r)
             for t in to_finish:
                 turn_att(t)
             for t in to_scale:
                 normalise(t)
-            turn_e(r)
+            if r > LAST_OWED:
+                turn_e(r)
             group_e(r)
             scores(r + HEAD_TILES)
             for b, piece in pieces_before:

from contextlib import ExitStack

import concourse.mybir as mybir
from concourse.masks import make_identity

F32 = mybir.dt.float32
BF16 = mybir.dt.bfloat16
U32 = mybir.dt.uint32
U8 = mybir.dt.uint8
FP8X4 = mybir.dt.float8_e4m3fn_x4
ALU = mybir.AluOpType
ACT = mybir.ActivationFunctionType
AXIS_X = mybir.AxisListType.X

B, C, D, N = 2, 512, 128, 1024
P = 128
PACK = 4
PAIR = 2
HALVES = PACK // PAIR
K_PASS = P * PACK
BANK = 512
C_TILES = C // P
M_TILES = N // P
TILES = B * M_TILES
KEY_PASSES = N // K_PASS
KEY_BANKS = N // BANK
PIECES = KEY_PASSES * C_TILES
STORE_TILES = 2
FIRST_Q = 2
FIRST_ATTEND = 5
TURN_ROUND = 2
E_LAG = 3
LAST_OWED = TILES - 2
HEAD_TILES = 2
VALUE_ROUNDS = 4
FLOPS = 2 * B * (C * C * N + N * D * N + C * N * N)


def tile_mvpam_module_mask_cascade_pb_kernel(tc, x, out1, q, k, wv2, bv2, gamma, out):
    nc = tc.nc
    with ExitStack() as ctx:
        ctx.enter_context(tc.manual_schedule())
        const = ctx.enter_context(tc.tile_pool(name="const", bufs=1))
        per_batch = ctx.enter_context(tc.tile_pool(name="per_batch", bufs=B))
        halves = ctx.enter_context(tc.tile_pool(name="halves", bufs=B * KEY_PASSES))
        work = ctx.enter_context(tc.tile_pool(name="work", bufs=6))
        ps_scores = ctx.enter_context(tc.psum_pool(name="ps_scores", bufs=2))
        ps_turn = ctx.enter_context(tc.psum_pool(name="ps_turn", bufs=2))
        ps_mx = ctx.enter_context(tc.psum_pool(name="ps_mx", bufs=2))

        q_sb, k_sb, x_sb = [], [], []
        o1_sb = {}

        def load_queries(b, first, last):
            if first == 0:
                q_rows = per_batch.tile([P, M_TILES, D], BF16)
                q_sb.append(q_rows)
            nc.sync.dma_start(
                out=q_sb[b][:, first:last, :], in_=q[b].rearrange("(i p) d -> p i d", p=P)[:, first:last, :]
            )

        def load_keys(b):
            k_rows = per_batch.tile([P, N], BF16)
            nc.sync.dma_start(out=k_rows[:], in_=k[b])
            k_sb.append(k_rows)

        def load_out1(b, g):
            o1_rows = halves.tile([P, PACK, K_PASS], BF16)
            o1_sb[b, g] = o1_rows
            keys = slice(g * K_PASS, (g + 1) * K_PASS)
            for j in range(HALVES):
                nc.sync.dma_start(
                    out=o1_rows[:, j * PAIR : (j + 1) * PAIR, :],
                    in_=out1[b].rearrange("(j p e) n -> j p e n", p=P, e=PAIR)[j, :, :, keys],
                )

        def load_x(b):
            x_rows = per_batch.tile([P, C_TILES, N], BF16)
            nc.sync.dma_start(out=x_rows[:], in_=x[b].rearrange("(ct p) m -> p ct m", p=P))
            x_sb.append(x_rows)

        load_queries(0, 0, FIRST_Q)
        load_keys(0)
        load_out1(0, 0)
        load_queries(0, FIRST_Q, M_TILES)
        w_sb = const.tile([P, C_TILES, C], BF16)
        nc.sync.dma_start(out=w_sb[:], in_=wv2.rearrange("(ct p) ci -> p ct ci", p=P))
        load_out1(0, 1)
        bias_bc = const.tile([P, C], BF16)
        nc.sync.dma_start(out=bias_bc[:], in_=bv2.partition_broadcast(P))
        gamma_bf = const.tile([P, 1], BF16)
        nc.sync.dma_start(out=gamma_bf[:], in_=gamma.partition_broadcast(P))
        load_out1(1, 0)
        load_queries(1, 0, M_TILES)
        load_keys(1)
        load_out1(1, 1)
        load_x(0)
        load_x(1)

        ident_bf = const.tile([P, P], BF16)
        make_identity(nc, ident_bf[:])
        ident_f32 = const.tile([P, P], F32)
        make_identity(nc, ident_f32[:])
        zero_col = const.tile([P, 1], F32)
        nc.vector.memset(zero_col[:], 0.0)
        one_col = const.tile([P, 1], F32)
        nc.scalar.activation(out=one_col[:], in_=zero_col[:], func=ACT.Exp)

        qT_sb = []

        def turn_queries(b, first, last):
            if first == 0:
                qT = per_batch.tile([P, N], BF16)
                qT_sb.append(qT)
            qT_ps = ps_turn.tile([P, M_TILES, P], BF16, tag="turn")
            for i in range(first, last):
                nc.tensor.transpose(qT_ps[:, i, :], q_sb[b][:, i, :], ident_bf[:])
            nc.scalar.copy(
                out=qT_sb[b][:, first * P : last * P],
                in_=qT_ps[:, first:last, :].rearrange("d i m -> d (i m)"),
            )

        w_grp = const.tile([P, C, HALVES], F32, align_bytes=64)
        w_codes = const.tile([P, C], U32, align_bytes=64)
        w_scales = const.tile([P, C], U8, align_bytes=64)

        def turn_weights(copies):
            per_bank = BANK // (HALVES * P)
            for first in range(0, C_TILES, per_bank):
                wT_ps = ps_turn.tile([P, per_bank, HALVES, P], F32, tag="turn")
                for a in range(per_bank):
                    w_words = w_sb[:, first + a, :].bitcast(F32)
                    for j in range(HALVES):
                        nc.tensor.transpose(
                            wT_ps[:, a, j, :], w_words[:, j * P : (j + 1) * P], ident_f32[:]
                        )
                copies[first // per_bank](
                    out=w_grp[:, first * P : (first + per_bank) * P, :].rearrange(
                        "p (a c) j -> p a c j", a=per_bank
                    ),
                    in_=wT_ps[:].rearrange("p a j c -> p a c j"),
                )

        def quantise_weights():
            nc.vector.quantize_mx(
                out=w_codes[:].bitcast(FP8X4),
                scales=w_scales[:],
                in_=w_grp[:].rearrange("p c j -> p (c j)").bitcast(BF16),
            )

        values = []
        for b in range(B):
            o1_grp = per_batch.tile([P, N, PACK], BF16, align_bytes=64)
            o1_codes = per_batch.tile([P, N], U32, align_bytes=64)
            o1_scales = per_batch.tile([P, N], U8, align_bytes=64)
            v_grp = per_batch.tile([P, KEY_PASSES, C, PACK], BF16, align_bytes=64)
            v_codes = per_batch.tile([P, KEY_PASSES, C], U32, align_bytes=64)
            v_scales = per_batch.tile([P, KEY_PASSES, C], U8, align_bytes=64)
            values.append(
                {
                    "o1_grp": o1_grp,
                    "o1_codes": o1_codes,
                    "o1_scales": o1_scales,
                    "v_grp": v_grp,
                    "v_codes": v_codes,
                    "v_scales": v_scales,
                }
            )
        vT_banks = {}

        def regroup_out1(b, g, j, e, copy):
            keys = slice(g * K_PASS + j * PAIR * P, g * K_PASS + (j + 1) * PAIR * P)
            copy(
                out=values[b]["o1_grp"][:, keys, :].rearrange("p (e q) u -> p e q u", e=PAIR)[:, e],
                in_=o1_sb[b, g][:, :, j * PAIR * P : (j + 1) * PAIR * P].rearrange("p u (q e) -> p e q u", e=PAIR)[:, e],
            )

        def gpsimd_copy(out, in_):
            nc.gpsimd.tensor_scalar(
                out=out, in0=in_, scalar1=1.0, scalar2=0.0, op0=ALU.mult, op1=ALU.add
            )

        def quantise_out1(b, g):
            keys = slice(g * K_PASS, (g + 1) * K_PASS)
            nc.vector.quantize_mx(
                out=values[b]["o1_codes"][:, keys].bitcast(FP8X4),
                scales=values[b]["o1_scales"][:, keys],
                in_=values[b]["o1_grp"][:, keys, :].rearrange("p n u -> p (n u)"),
            )

        def values_matmul(b, piece):
            if not 0 <= piece < PIECES:
                return
            g, cb = divmod(piece, C_TILES)
            chans = slice(cb * P, (cb + 1) * P)
            vT_ps = ps_mx.tile([P, PACK, P], F32, tag="mx")
            for u in range(PACK):
                key_tile = slice(g * K_PASS + u * P, g * K_PASS + (u + 1) * P)
                nc.tensor.matmul_mx(
                    out=vT_ps[:, u, :],
                    lhsT=values[b]["o1_codes"][:, key_tile].bitcast(FP8X4),
                    lhsT_scale=values[b]["o1_scales"][:, key_tile],
                    rhs=w_codes[:, chans].bitcast(FP8X4),
                    rhs_scale=w_scales[:, chans],
                    start=True,
                    stop=True,
                )
            vT_banks[b, piece] = vT_ps

        def values_add_bias(b, piece):
            if not 0 <= piece < PIECES:
                return
            g, cb = divmod(piece, C_TILES)
            chans = slice(cb * P, (cb + 1) * P)
            nc.vector.tensor_tensor(
                out=values[b]["v_grp"][:, g, chans, :],
                in0=vT_banks[b, piece][:].rearrange("p u c -> p c u"),
                in1=bias_bc[:, chans].unsqueeze(2).to_broadcast([P, P, PACK]),
                op=ALU.add,
            )

        def values_quantise(b, piece):
            if not 0 <= piece < PIECES:
                return
            g, cb = divmod(piece, C_TILES)
            if cb < C_TILES - 1:
                return
            nc.vector.quantize_mx(
                out=values[b]["v_codes"][:, g, :].bitcast(FP8X4),
                scales=values[b]["v_scales"][:, g, :],
                in_=values[b]["v_grp"][:, g, :, :].rearrange("p c u -> p (c u)"),
            )

        live = {}

        def scores(t):
            if not 0 <= t < TILES:
                return
            b, i = divmod(t, M_TILES)
            s_ps = ps_scores.tile([P, KEY_BANKS, BANK], F32, tag="scores")
            for h in range(KEY_BANKS):
                nc.tensor.matmul(
                    out=s_ps[:, h, :],
                    lhsT=qT_sb[b][:, i * P : (i + 1) * P],
                    rhs=k_sb[b][:, h * BANK : (h + 1) * BANK],
                    start=True,
                    stop=True,
                )
            live["s", t] = s_ps

        def row_max(t):
            if not 0 <= t < TILES:
                return
            bank_max = work.tile([P, KEY_BANKS], F32)
            for h in range(KEY_BANKS):
                nc.vector.tensor_reduce(
                    out=bank_max[:, h : h + 1], in_=live["s", t][:, h, :], axis=AXIS_X, op=ALU.max
                )
            neg_max = work.tile([P, 1], F32)
            nc.gpsimd.tensor_scalar(
                out=neg_max[:],
                in0=bank_max[:, 0:1],
                scalar1=bank_max[:, 1:2],
                scalar2=-1.0,
                op0=ALU.max,
                op1=ALU.mult,
            )
            live["neg_max", t] = neg_max

        def exponentials(t):
            if not 0 <= t < TILES:
                return
            e_sb = work.tile([P, N], BF16)
            bank_sum = work.tile([P, KEY_BANKS], F32)
            for h in range(KEY_BANKS):
                nc.scalar.activation(
                    out=e_sb[:, h * BANK : (h + 1) * BANK],
                    in_=live["s", t][:, h, :],
                    func=ACT.Exp,
                    bias=live["neg_max", t][:],
                    scale=1.0,
                    accum_out=bank_sum[:, h : h + 1],
                )
            if t % 2 == 0:
                row_sums = work.tile([P, 2], F32)
                live["row_sums", t // 2] = row_sums
            nc.gpsimd.tensor_tensor(
                out=live["row_sums", t // 2][:, t % 2 : t % 2 + 1],
                in0=bank_sum[:, 0:1],
                in1=bank_sum[:, 1:2],
                op=ALU.add,
            )
            live["e", t] = e_sb

        def turn_e(t):
            if not 0 <= t < TILES:
                return
            e_words = live["e", t][:].bitcast(F32)
            eT_ps = ps_turn.tile([P, KEY_PASSES * HALVES, P], F32, tag="turn")
            for gj in range(KEY_PASSES * HALVES):
                nc.tensor.transpose(eT_ps[:, gj, :], e_words[:, gj * P : (gj + 1) * P], ident_f32[:])
            live["eT", t] = eT_ps

        def group_e(t):
            if not 0 <= t < TILES:
                return
            e_grp = work.tile([P, KEY_PASSES, P, HALVES], F32, align_bytes=64)
            nc.scalar.copy(
                out=e_grp[:], in_=live["eT", t][:].rearrange("p (g j) m -> p g m j", g=KEY_PASSES)
            )
            live["e_grp", t] = e_grp

        def quantise_e(t):
            if not 0 <= t < TILES:
                return
            e_codes = work.tile([P, KEY_PASSES, P], U32, align_bytes=64)
            e_scales = work.tile([P, KEY_PASSES, P], U8, align_bytes=64)
            nc.vector.quantize_mx(
                out=e_codes[:].rearrange("p g m -> p (g m)").bitcast(FP8X4),
                scales=e_scales[:].rearrange("p g m -> p (g m)"),
                in_=live["e_grp", t][:].rearrange("p g m j -> p (g m j)").bitcast(BF16),
            )
            live["e_codes", t] = e_codes
            live["e_scales", t] = e_scales

        def invert_sum(t):
            if not 0 <= t < TILES:
                return
            if t % 2 == 0:
                return
            inv_sums = work.tile([P, 2], F32)
            nc.vector.reciprocal(out=inv_sums[:], in_=live["row_sums", t // 2][:])
            for n in range(2):
                live["inv_sum", t - 1 + n] = inv_sums[:, n : n + 1]

        def attend(t):
            if not 0 <= t < TILES:
                return
            b = t // M_TILES
            if t >= 11 and t % 2 == 1:
                s_ps = ps_scores.tile([P, KEY_BANKS, BANK], F32, tag="scores")
                attT_ps = s_ps[:, 0, :]
            else:
                mx_ps = ps_mx.tile([P, C], F32, tag="mx")
                attT_ps = mx_ps[:]
            for g in range(KEY_PASSES):
                nc.tensor.matmul_mx(
                    out=attT_ps,
                    lhsT=live["e_codes", t][:, g, :].bitcast(FP8X4),
                    lhsT_scale=live["e_scales", t][:, g, :],
                    rhs=values[b]["v_codes"][:, g, :].bitcast(FP8X4),
                    rhs_scale=values[b]["v_scales"][:, g, :],
                    start=(g == 0),
                    stop=(g == KEY_PASSES - 1),
                )
            live["attT_ps", t] = attT_ps

        def normalise(t):
            if not 0 <= t < TILES:
                return
            attT_sb = work.tile([P, C], F32)
            nc.scalar.activation(
                out=attT_sb[:], in_=live["attT_ps", t], func=ACT.Copy, scale=live["inv_sum", t]
            )
            live["attT_sb", t] = attT_sb

        def turn_att(t):
            if not 0 <= t < TILES:
                return
            if t >= 14:
                s_ps = ps_scores.tile([P, KEY_BANKS, BANK], F32, tag="scores")
                att_ps = s_ps[:, 0, :].rearrange("p (ct m) -> p ct m", ct=C_TILES)
            else:
                turn_ps = ps_turn.tile([P, C_TILES, P], F32, tag="turn")
                att_ps = turn_ps[:]
            for ct in range(C_TILES):
                nc.tensor.transpose(
                    att_ps[:, ct, :], live["attT_sb", t][:, ct * P : (ct + 1) * P], ident_f32[:]
                )
            live["att", t] = att_ps

        def finish(t):
            if not 0 <= t < TILES:
                return
            b, i = divmod(t, M_TILES)
            part = i % STORE_TILES
            if part == 0:
                out_sb = work.tile([P, C_TILES, STORE_TILES * P], F32)
                live["out", t // STORE_TILES] = out_sb
            out_sb = live["out", t // STORE_TILES]
            nc.vector.scalar_tensor_tensor(
                out=out_sb[:, :, part * P : (part + 1) * P],
                in0=live["att", t],
                scalar=gamma_bf[:],
                in1=x_sb[b][:, :, i * P : (i + 1) * P],
                op0=ALU.mult,
                op1=ALU.add,
            )
            stored = 1 if t >= TILES - STORE_TILES else STORE_TILES
            if (part + 1) % stored == 0:
                cols = slice((part + 1 - stored) * P, (part + 1) * P)
                first = (i + 1 - stored) * P
                nc.sync.dma_start(
                    out=out[b].rearrange("(ct p) m -> p ct m", p=P)[:, :, first : first + stored * P],
                    in_=out_sb[:, :, cols],
                )

        all_e = slice(0, PAIR)
        turn_queries(0, 0, FIRST_Q)
        scores(0)
        scores(1)
        regroup_out1(0, 0, 0, all_e, nc.vector.tensor_copy)
        for e in range(PAIR):
            regroup_out1(0, 0, 1, slice(e, e + 1), nc.scalar.copy)
        row_max(0)
        row_max(1)
        quantise_out1(0, 0)
        turn_queries(0, FIRST_Q, M_TILES)
        turn_weights((nc.vector.tensor_copy, nc.vector.tensor_copy))
        for j in range(HALVES):
            for e in range(PAIR):
                regroup_out1(0, 1, j, slice(e, e + 1), gpsimd_copy)
        quantise_weights()

        attended = 0
        scaled = 0
        turned = 0
        quantised = 0
        pieces_before = []
        held = []
        for r in range(TILES + HEAD_TILES + 2):
            if r < VALUE_ROUNDS:
                pieces = [(0, 2 * r), (0, 2 * r + 1)]
            elif r - VALUE_ROUNDS < PIECES:
                pieces = [(1, r - VALUE_ROUNDS)]
            else:
                pieces = []
            at_once = 0 if r < FIRST_ATTEND else 1 if r + HEAD_TILES < TILES else 2
            now = range(attended, min(attended + at_once, TILES))
            to_scale = range(scaled, attended)
            to_finish = range(turned, scaled)
            turned, scaled, attended = scaled, attended, attended + len(now)

            if r > LAST_OWED:
                quantise_e(r - 1)
                invert_sum(r - 1)
            exponentials(r)
            if r == TURN_ROUND:
                turn_queries(1, 0, M_TILES)
            for b, piece in held:
                values_matmul(b, piece)
            if r <= LAST_OWED:
                turn_e(r)
            for t in to_finish:
                turn_att(t)
            for t in to_scale:
                normalise(t)
            if r > LAST_OWED:
                turn_e(r)
            group_e(r)
            scores(r + HEAD_TILES)
            for b, piece in pieces_before:
                values_add_bias(b, piece)
            for t in to_finish:
                finish(t)
            row_max(r + HEAD_TILES)
            if r <= LAST_OWED:
                for t in range(quantised, r if r == LAST_OWED else r - E_LAG + 1):
                    quantise_e(t)
                    quantised = t + 1
                invert_sum(r - 1)
            for b, piece in pieces_before:
                values_quantise(b, piece)
            for t in now:
                attend(t)
            held = pieces if r == TURN_ROUND - 1 else []
            if not held:
                for b, piece in pieces:
                    values_matmul(b, piece)
            pieces_before = pieces
            if 1 <= r <= KEY_PASSES * HALVES:
                g, j = divmod(r - 1, HALVES)
                for e in range(PAIR):
                    regroup_out1(1, g, j, slice(e, e + 1), gpsimd_copy)
            if r == 0:
                quantise_out1(0, 1)
            if r == 3:
                quantise_out1(1, 0)
            if r == 6:
                quantise_out1(1, 1)
